import numpy as np
import ml_dtypes


def mxq(x, axis, fmt="e4m3"):
    dtype, down = {"e4m3": (ml_dtypes.float8_e4m3fn, 7), "e5m2": (ml_dtypes.float8_e5m2, 14)}[fmt]
    v = np.moveaxis(np.asarray(x, np.float32).astype(ml_dtypes.bfloat16).astype(np.float64), axis, -1)
    blocks = v.reshape(v.shape[:-1] + (-1, 32))
    amax = np.abs(blocks).max(-1, keepdims=True)
    byte = np.maximum(np.where(amax > 0, np.frexp(amax)[1] - 1 + 127, 0) - down, 1)
    scale = np.exp2(byte - 127.0)
    codes = (blocks / scale).astype(np.float32).astype(dtype).astype(np.float64)
    return np.moveaxis((codes * scale).reshape(v.shape), -1, axis)


WIDE = False


def mx_kscale(k):
    if not WIDE:
        return np.ones(k)
    levels = np.array([10, -10, 5, -5, 0])
    a = np.random.permutation(np.resize(levels, k // 512 * 4)).reshape(k // 512, 4)
    idx = np.arange(k)
    return np.exp2(a[idx // 512, idx % 128 // 32])


BF16 = ml_dtypes.bfloat16


def bf(x):
    return np.asarray(x, np.float32).astype(BF16)


def f64(x):
    return np.asarray(x).astype(np.float64)


B, H0, H1, H2 = 8192, 512, 512, 128
NEG_SLOPE = 0.01
LV_MIN, LV_MAX = -10.0, 10.0


def leaky_relu(v):
    return np.where(v > 0, v, NEG_SLOPE * v)


def setup_inputs():
    s = mx_kscale(H0)
    t = mx_kscale(H1)
    return {"x": bf(np.random.standard_normal((B, H0)) * s),
            "noise_enc": bf(np.random.standard_normal((B, H2))),
            "noise_z": bf(np.random.standard_normal((B, H2))),
            "w1_mu": bf(np.random.standard_normal((H0, H1)) / np.sqrt(H0) / s[:, None] * t),
            "b1_mu": bf(np.random.standard_normal(H1) * 0.5 * t),
            "w2_mu": bf(np.random.standard_normal((H1, H2)) * 6.0 / np.sqrt(H1) / t[:, None]),
            "b2_mu": bf(np.random.standard_normal(H2) * 1.0),
            "w1_sig": bf(np.random.standard_normal((H0, H1)) / np.sqrt(H0) / s[:, None]),
            "b1_sig": bf(np.random.standard_normal(H1) * 0.3),
            "w2_sig": bf(np.random.standard_normal((H1, H2)) * 4.5 / np.sqrt(H1)),
            "b2_sig": bf(np.random.standard_normal(H2) * 0.8)}


def reference(x, noise_enc, noise_z, w1_mu, b1_mu, w2_mu, b2_mu, w1_sig, b1_sig, w2_sig, b2_sig):
    xq = mxq(f64(x), 1, "e4m3")
    h_mu = leaky_relu((xq @ mxq(f64(w1_mu), 0, "e4m3")) + f64(b1_mu))
    mean = leaky_relu((mxq(h_mu, 1, "e4m3") @ mxq(f64(w2_mu), 0, "e4m3")) + f64(b2_mu))
    h_sig = np.tanh((xq @ mxq(f64(w1_sig), 0, "e4m3")) + f64(b1_sig))
    log_var = leaky_relu((mxq(h_sig, 1, "e4m3") @ mxq(f64(w2_sig), 0, "e4m3")) + f64(b2_sig))
    log_var = np.clip(log_var, LV_MIN, LV_MAX)
    std = np.exp(0.5 * log_var)
    z_enc = mean + std * f64(noise_enc)
    z = mean + std * f64(noise_z)
    return z_enc, z

@@ -1,0 +1,238 @@
+from contextlib import ExitStack
+
+import concourse.mybir as mybir
+from concourse.masks import make_identity
+
+F32 = mybir.dt.float32
+BF16 = mybir.dt.bfloat16
+U32 = mybir.dt.uint32
+U8 = mybir.dt.uint8
+FP8X4 = mybir.dt.float8_e4m3fn_x4
+ACT = mybir.ActivationFunctionType
+ALU = mybir.AluOpType
+
+P = 128
+PACK = 4
+BATCH, FEATURES, HIDDEN, LATENT = 8192, 512, 512, 128
+CHUNK = 512
+ROW_TILES = CHUNK // P
+N_CHUNKS = BATCH // CHUNK
+HIDDEN_TILES = HIDDEN // P
+NEG_SLOPE = 0.01
+LV_MIN, LV_MAX = -10.0, 10.0
+
+SCALAR_COLS = 192
+
+FLOPS = 2 * BATCH * 2 * (FEATURES * HIDDEN + HIDDEN * LATENT)
+
+
+def quantise_weight(nc, stage, keep, w, cols, name, spread):
+    raw = stage.tile([P, PACK, cols], BF16, name=name + "_raw")
+    nc.sync.dma_start(out=raw[:], in_=w.rearrange("(p j) n -> p j n", j=PACK))
+    grouped = stage.tile([P, cols, PACK], BF16, name=name + "_grouped", align_bytes=64)
+    if spread:
+        nc.vector.tensor_copy(
+            out=grouped[:].rearrange("p (m q) j -> p m q j", q=P),
+            in_=raw[:].rearrange("p j (q m) -> p m q j", q=P),
+        )
+    else:
+        nc.vector.tensor_copy(out=grouped[:], in_=raw[:].rearrange("p j n -> p n j"))
+    codes = keep.tile([P, cols], U32, name=name + "_codes", align_bytes=64)
+    scales = keep.tile([P, cols], U8, name=name + "_scales", align_bytes=64)
+    nc.vector.quantize_mx(
+        out=codes[:].bitcast(FP8X4),
+        scales=scales[:],
+        in_=grouped[:].rearrange("p n j -> p (n j)"),
+    )
+    return codes, scales
+
+
+def load_bias(nc, stage, keep, b, per_partition, name):
+    raw = stage.tile([P, per_partition], BF16, name=name + "_raw")
+    nc.sync.dma_start(out=raw[:], in_=b.rearrange("(p m) -> p m", m=per_partition))
+    bias = keep.tile([P, per_partition], F32, name=name)
+    nc.vector.tensor_copy(out=bias[:], in_=raw[:])
+    return bias
+
+
+def quantise(nc, pool, grouped, name):
+    codes = pool.tile([P, CHUNK], U32, name=name + "_codes", align_bytes=64)
+    scales = pool.tile([P, CHUNK], U8, name=name + "_scales", align_bytes=64)
+    nc.vector.quantize_mx(
+        out=codes[:].bitcast(FP8X4),
+        scales=scales[:],
+        in_=grouped[:].rearrange("p b j -> p (b j)"),
+    )
+    return codes, scales
+
+
+def mx_pass(nc, acc, weight, w_cols, moving):
+    nc.tensor.matmul_mx(
+        out=acc[:],
+        lhsT=weight[0][:, w_cols].bitcast(FP8X4),
+        lhsT_scale=weight[1][:, w_cols],
+        rhs=moving[0][:].bitcast(FP8X4),
+        rhs_scale=moving[1][:],
+        start=True,
+        stop=True,
+    )
+
+
+def leaky(nc, out, y):
+    nc.vector.scalar_tensor_tensor(out=out, in0=y, scalar=NEG_SLOPE, in1=y, op0=ALU.mult, op1=ALU.max)
+
+
+def side_by_side(planes, grouped, cols):
+    return (
+        grouped[:, cols, :].rearrange("p (c i) j -> p c j i", i=4),
+        planes[:, :, cols].rearrange("p j (c i) -> p c j i", i=4),
+    )
+
+
+def tile_infovae_pa_t_kernel(
+    tc, x, noise_enc, noise_z, w1_mu, b1_mu, w2_mu, b2_mu, w1_sig, b1_sig, w2_sig, b2_sig, out_0, out_1
+):
+    nc = tc.nc
+    x_chunks = x.rearrange("(p c t) k -> c p (t k)", c=N_CHUNKS, t=ROW_TILES)
+    noise_chunks = [
+        n.rearrange("(p c t) h -> c p (t h)", c=N_CHUNKS, t=ROW_TILES) for n in (noise_enc, noise_z)
+    ]
+    out_chunks = [o.rearrange("(p c t) h -> c p (t h)", c=N_CHUNKS, t=ROW_TILES) for o in (out_0, out_1)]
+
+    with ExitStack() as ctx:
+        keep = ctx.enter_context(tc.tile_pool(name="keep", bufs=1))
+        stage = ctx.enter_context(tc.tile_pool(name="stage", bufs=1))
+        loads = ctx.enter_context(tc.tile_pool(name="loads", bufs=3))
+        noises = ctx.enter_context(tc.tile_pool(name="noises", bufs=6))
+        work = ctx.enter_context(tc.tile_pool(name="work", bufs=2))
+        psum_x = ctx.enter_context(tc.psum_pool(name="psum_x", bufs=2))
+        psum_h = ctx.enter_context(tc.psum_pool(name="psum_h", bufs=3))
+        psum_o = ctx.enter_context(tc.psum_pool(name="psum_o", bufs=1))
+        ctx.enter_context(tc.manual_schedule())
+
+        x_rows, noise, x_q, h_mu_q, h_sig_q, mean_t, lv_clipped, std_t = {}, {}, {}, {}, {}, {}, {}, {}
+
+        def load(c):
+            x_rows[c] = loads.tile([P, ROW_TILES * FEATURES], BF16, name="x_rows")
+            nc.sync.dma_start(out=x_rows[c][:], in_=x_chunks[c])
+            noise[c] = noises.tile([P, 2, CHUNK], BF16, name="noise")
+            for s in range(2):
+                nc.sync.dma_start(out=noise[c][:, s, :], in_=noise_chunks[s][c])
+
+        def transpose_x(c):
+            x_words = x_rows[c][:].bitcast(F32)
+            x_grouped = work.tile([P, CHUNK, PACK], BF16, name="x_grouped", align_bytes=64)
+            x_grouped_words = x_grouped[:].rearrange("p b j -> p (b j)").bitcast(F32)
+            words = FEATURES // 2
+            for pair in range(2):
+                x_t = psum_x.tile([P, 2, CHUNK // 2], F32, name="x_t")
+                for tt in range(2):
+                    t = 2 * pair + tt
+                    for u in range(2):
+                        nc.tensor.transpose(
+                            x_t[:, u, tt * P : (tt + 1) * P],
+                            x_words[:, t * words + u : (t + 1) * words : 2],
+                            identity[:],
+                        )
+                nc.scalar.copy(
+                    out=x_grouped_words[:, pair * CHUNK : (pair + 1) * CHUNK].rearrange(
+                        "p (b u) -> p b u", u=2
+                    ),
+                    in_=x_t[:].rearrange("p u b -> p b u"),
+                )
+            return x_grouped
+
+        def hidden(c):
+            y_mu = work.tile([P, HIDDEN_TILES, CHUNK], F32, name="y_mu")
+            h_sig = work.tile([P, HIDDEN_TILES, CHUNK], BF16, name="h_sig")
+            for m in range(HIDDEN_TILES):
+                acc = psum_h.tile([P, CHUNK], F32, name="acc")
+                mx_pass(nc, acc, w1_mu_q, slice(m * P, (m + 1) * P), x_q[c])
+                nc.scalar.activation(
+                    out=y_mu[:, m, :], in_=acc[:], func=ACT.Identity, bias=b1_mu_f[:, m : m + 1], scale=1.0
+                )
+            for m in range(HIDDEN_TILES):
+                acc = psum_h.tile([P, CHUNK], F32, name="acc")
+                mx_pass(nc, acc, w1_sig_q, slice(m * P, (m + 1) * P), x_q[c])
+                nc.scalar.activation(
+                    out=h_sig[:, m, :], in_=acc[:], func=ACT.Tanh, bias=b1_sig_f[:, m : m + 1], scale=1.0
+                )
+            return y_mu, h_sig
+
+        def output_layers(c):
+            y_out = work.tile([P, 2, CHUNK], F32, name="y_out")
+            for s, (w, h, b) in enumerate(((w2_mu_q, h_mu_q[c], b2_mu_f), (w2_sig_q, h_sig_q[c], b2_sig_f))):
+                acc = psum_o.tile([P, CHUNK], F32, name="acc_o")
+                mx_pass(nc, acc, w, slice(0, LATENT), h)
+                nc.scalar.activation(out=y_out[:, s, :], in_=acc[:], func=ACT.Identity, bias=b[:, 0:1], scale=1.0)
+            return y_out
+
+        def samples(c):
+            mean = psum_o.tile([P, CHUNK], F32, name="mean")
+            std = psum_o.tile([P, CHUNK], F32, name="std")
+            for back, turned in ((std, std_t[c]), (mean, mean_t[c])):
+                for t in range(ROW_TILES):
+                    cols = slice(t * P, (t + 1) * P)
+                    nc.tensor.transpose(back[:, cols], turned[:, cols], identity[:])
+            z = work.tile([P, 2, CHUNK], F32, name="z")
+            nc.vector.tensor_tensor(
+                out=z[:], in0=std[:].unsqueeze(1).to_broadcast([P, 2, CHUNK]), in1=noise[c][:], op=ALU.mult
+            )
+            nc.vector.tensor_tensor(
+                out=z[:], in0=z[:], in1=mean[:].unsqueeze(1).to_broadcast([P, 2, CHUNK]), op=ALU.add
+            )
+            for s in range(2):
+                nc.sync.dma_start(out=out_chunks[s][c], in_=z[:, s, :])
+
+        load(0)
+        identity = keep.tile([P, P], F32, name="identity")
+        make_identity(nc, identity[:])
+        zero = keep.tile([P, 1], F32, name="zero")
+        nc.vector.memset(zero[:], 0.0)
+        warm = keep.tile([P, 1], F32, name="warm")
+        nc.scalar.activation(out=warm[:], in_=zero[:], func=ACT.Tanh)
+
+        w1_mu_q = quantise_weight(nc, stage, keep, w1_mu, HIDDEN, "w1_mu", True)
+        b1_mu_f = load_bias(nc, stage, keep, b1_mu, HIDDEN_TILES, "b1_mu")
+        w1_sig_q = quantise_weight(nc, stage, keep, w1_sig, HIDDEN, "w1_sig", True)
+        b1_sig_f = load_bias(nc, stage, keep, b1_sig, HIDDEN_TILES, "b1_sig")
+        load(1)
+        w2_mu_q = quantise_weight(nc, stage, keep, w2_mu, LATENT, "w2_mu", False)
+        b2_mu_f = load_bias(nc, stage, keep, b2_mu, 1, "b2_mu")
+        w2_sig_q = quantise_weight(nc, stage, keep, w2_sig, LATENT, "w2_sig", False)
+        b2_sig_f = load_bias(nc, stage, keep, b2_sig, 1, "b2_sig")
+
+        for i in range(-1, N_CHUNKS + 2):
+            if 0 <= i and i + 2 < N_CHUNKS:
+                load(i + 2)
+            if 0 <= i < N_CHUNKS:
+                y_mu, h_sig = hidden(i)
+                h_sig_grouped = work.tile([P, CHUNK, PACK], BF16, name="h_sig_grouped", align_bytes=64)
+                to_s, from_s = side_by_side(h_sig, h_sig_grouped, slice(0, SCALAR_COLS))
+                nc.scalar.copy(out=to_s, in_=from_s)
+            if i + 1 < N_CHUNKS:
+                x_grouped = transpose_x(i + 1)
+            if 0 <= i < N_CHUNKS:
+                h_mu_grouped = work.tile([P, CHUNK, PACK], BF16, name="h_mu_grouped", align_bytes=64)
+                leaky(nc, h_mu_grouped[:], y_mu[:].rearrange("p m b -> p b m"))
+                to_v, from_v = side_by_side(h_sig, h_sig_grouped, slice(SCALAR_COLS, CHUNK))
+                nc.vector.tensor_copy(out=to_v, in_=from_v)
+            if i + 1 < N_CHUNKS:
+                x_q[i + 1] = quantise(nc, work, x_grouped, "x")
+            if 0 <= i < N_CHUNKS:
+                h_mu_q[i] = quantise(nc, work, h_mu_grouped, "h_mu")
+                h_sig_q[i] = quantise(nc, work, h_sig_grouped, "h_sig")
+            if 0 <= i - 1 < N_CHUNKS:
+                y_out = output_layers(i - 1)
+                l_out = work.tile([P, 2, CHUNK], F32, name="l_out")
+                leaky(nc, l_out[:], y_out[:])
+                mean_t[i - 1] = l_out[:, 0, :]
+                lv_clipped[i - 1] = work.tile([P, CHUNK], F32, name="lv_clipped")
+                nc.vector.tensor_scalar(
+                    out=lv_clipped[i - 1][:], in0=l_out[:, 1, :], scalar1=LV_MAX, scalar2=LV_MIN,
+                    op0=ALU.min, op1=ALU.max,
+                )
+            if 0 <= i - 2:
+                std_t[i - 2] = work.tile([P, CHUNK], F32, name="std_t")
+                nc.scalar.activation(out=std_t[i - 2][:], in_=lv_clipped[i - 2][:], func=ACT.Exp, scale=0.5)
+                samples(i - 2)

@@ -103,12 +103,11 @@ def tile_infovae_pa_t_kernel(
         keep = ctx.enter_context(tc.tile_pool(name="keep", bufs=1))
         stage = ctx.enter_context(tc.tile_pool(name="stage", bufs=1))
         loads = ctx.enter_context(tc.tile_pool(name="loads", bufs=3))
-        noises = ctx.enter_context(tc.tile_pool(name="noises", bufs=6))
-        work = ctx.enter_context(tc.tile_pool(name="work", bufs=2))
+        noises = ctx.enter_context(tc.tile_pool(name="noises", bufs=4))
+        work = ctx.enter_context(tc.tile_pool(name="work", bufs=3))
         psum_x = ctx.enter_context(tc.psum_pool(name="psum_x", bufs=2))
         psum_h = ctx.enter_context(tc.psum_pool(name="psum_h", bufs=3))
         psum_o = ctx.enter_context(tc.psum_pool(name="psum_o", bufs=1))
-        ctx.enter_context(tc.manual_schedule())
 
         x_rows, noise, x_q, h_mu_q, h_sig_q, mean_t, lv_clipped, std_t = {}, {}, {}, {}, {}, {}, {}, {}
 
@@ -202,37 +201,32 @@ def tile_infovae_pa_t_kernel(
         w2_sig_q = quantise_weight(nc, stage, keep, w2_sig, LATENT, "w2_sig", False)
         b2_sig_f = load_bias(nc, stage, keep, b2_sig, 1, "b2_sig")
 
-        for i in range(-1, N_CHUNKS + 2):
-            if 0 <= i and i + 2 < N_CHUNKS:
-                load(i + 2)
-            if 0 <= i < N_CHUNKS:
-                y_mu, h_sig = hidden(i)
-                h_sig_grouped = work.tile([P, CHUNK, PACK], BF16, name="h_sig_grouped", align_bytes=64)
-                to_s, from_s = side_by_side(h_sig, h_sig_grouped, slice(0, SCALAR_COLS))
-                nc.scalar.copy(out=to_s, in_=from_s)
-            if i + 1 < N_CHUNKS:
-                x_grouped = transpose_x(i + 1)
-            if 0 <= i < N_CHUNKS:
-                h_mu_grouped = work.tile([P, CHUNK, PACK], BF16, name="h_mu_grouped", align_bytes=64)
-                leaky(nc, h_mu_grouped[:], y_mu[:].rearrange("p m b -> p b m"))
-                to_v, from_v = side_by_side(h_sig, h_sig_grouped, slice(SCALAR_COLS, CHUNK))
-                nc.vector.tensor_copy(out=to_v, in_=from_v)
-            if i + 1 < N_CHUNKS:
-                x_q[i + 1] = quantise(nc, work, x_grouped, "x")
-            if 0 <= i < N_CHUNKS:
-                h_mu_q[i] = quantise(nc, work, h_mu_grouped, "h_mu")
-                h_sig_q[i] = quantise(nc, work, h_sig_grouped, "h_sig")
-            if 0 <= i - 1 < N_CHUNKS:
-                y_out = output_layers(i - 1)
-                l_out = work.tile([P, 2, CHUNK], F32, name="l_out")
-                leaky(nc, l_out[:], y_out[:])
-                mean_t[i - 1] = l_out[:, 0, :]
-                lv_clipped[i - 1] = work.tile([P, CHUNK], F32, name="lv_clipped")
-                nc.vector.tensor_scalar(
-                    out=lv_clipped[i - 1][:], in0=l_out[:, 1, :], scalar1=LV_MAX, scalar2=LV_MIN,
-                    op0=ALU.min, op1=ALU.max,
-                )
-            if 0 <= i - 2:
-                std_t[i - 2] = work.tile([P, CHUNK], F32, name="std_t")
-                nc.scalar.activation(out=std_t[i - 2][:], in_=lv_clipped[i - 2][:], func=ACT.Exp, scale=0.5)
-                samples(i - 2)
+        for c in range(N_CHUNKS):
+            if c + 2 < N_CHUNKS:
+                load(c + 2)
+            x_grouped = transpose_x(c)
+            x_q[c] = quantise(nc, work, x_grouped, "x")
+
+            y_mu, h_sig = hidden(c)
+            h_mu_grouped = work.tile([P, CHUNK, PACK], BF16, name="h_mu_grouped", align_bytes=64)
+            leaky(nc, h_mu_grouped[:], y_mu[:].rearrange("p m b -> p b m"))
+            h_sig_grouped = work.tile([P, CHUNK, PACK], BF16, name="h_sig_grouped", align_bytes=64)
+            to_s, from_s = side_by_side(h_sig, h_sig_grouped, slice(0, SCALAR_COLS))
+            nc.scalar.copy(out=to_s, in_=from_s)
+            to_v, from_v = side_by_side(h_sig, h_sig_grouped, slice(SCALAR_COLS, CHUNK))
+            nc.vector.tensor_copy(out=to_v, in_=from_v)
+            h_mu_q[c] = quantise(nc, work, h_mu_grouped, "h_mu")
+            h_sig_q[c] = quantise(nc, work, h_sig_grouped, "h_sig")
+
+            y_out = output_layers(c)
+            l_out = work.tile([P, 2, CHUNK], F32, name="l_out")
+            leaky(nc, l_out[:], y_out[:])
+            mean_t[c] = l_out[:, 0, :]
+            lv_clipped[c] = work.tile([P, CHUNK], F32, name="lv_clipped")
+            nc.vector.tensor_scalar(
+                out=lv_clipped[c][:], in0=l_out[:, 1, :], scalar1=LV_MAX, scalar2=LV_MIN,
+                op0=ALU.min, op1=ALU.max,
+            )
+            std_t[c] = work.tile([P, CHUNK], F32, name="std_t")
+            nc.scalar.activation(out=std_t[c][:], in_=lv_clipped[c][:], func=ACT.Exp, scale=0.5)
+            samples(c)

@@ -102,26 +102,39 @@ def tile_infovae_pa_t_kernel(
     with ExitStack() as ctx:
         keep = ctx.enter_context(tc.tile_pool(name="keep", bufs=1))
         stage = ctx.enter_context(tc.tile_pool(name="stage", bufs=1))
-        loads = ctx.enter_context(tc.tile_pool(name="loads", bufs=3))
-        noises = ctx.enter_context(tc.tile_pool(name="noises", bufs=4))
-        work = ctx.enter_context(tc.tile_pool(name="work", bufs=3))
+        two = ctx.enter_context(tc.tile_pool(name="two", bufs=2))
+        three = ctx.enter_context(tc.tile_pool(name="three", bufs=3))
+        six = ctx.enter_context(tc.tile_pool(name="six", bufs=6))
         psum_x = ctx.enter_context(tc.psum_pool(name="psum_x", bufs=2))
         psum_h = ctx.enter_context(tc.psum_pool(name="psum_h", bufs=3))
         psum_o = ctx.enter_context(tc.psum_pool(name="psum_o", bufs=1))
+        ctx.enter_context(tc.manual_schedule())
 
-        x_rows, noise, x_q, h_mu_q, h_sig_q, mean_t, lv_clipped, std_t = {}, {}, {}, {}, {}, {}, {}, {}
+        x_rows, noise, x_grouped, x_q, y_mu, h_sig = {}, {}, {}, {}, {}, {}
+        h_mu_grouped, h_sig_grouped, h_mu_q, h_sig_q = {}, {}, {}, {}
+        y_out, l_out, lv_clipped, std_t, mean, std, z = {}, {}, {}, {}, {}, {}, {}
 
-        def load(c):
-            x_rows[c] = loads.tile([P, ROW_TILES * FEATURES], BF16, name="x_rows")
-            nc.sync.dma_start(out=x_rows[c][:], in_=x_chunks[c])
-            noise[c] = noises.tile([P, 2, CHUNK], BF16, name="noise")
-            for s in range(2):
-                nc.sync.dma_start(out=noise[c][:, s, :], in_=noise_chunks[s][c])
+        def live(c):
+            return 0 <= c < N_CHUNKS
 
-        def transpose_x(c):
+
+        def load_x(c):
+            if live(c):
+                x_rows[c] = three.tile([P, ROW_TILES * FEATURES], BF16, name="x_rows")
+                nc.sync.dma_start(out=x_rows[c][:], in_=x_chunks[c])
+
+        def load_noise(c):
+            if live(c):
+                noise[c] = six.tile([P, 2, CHUNK], BF16, name="noise")
+                for s in range(2):
+                    nc.sync.dma_start(out=noise[c][:, s, :], in_=noise_chunks[s][c])
+
+        def turn_x(c):
+            if not live(c):
+                return
             x_words = x_rows[c][:].bitcast(F32)
-            x_grouped = work.tile([P, CHUNK, PACK], BF16, name="x_grouped", align_bytes=64)
-            x_grouped_words = x_grouped[:].rearrange("p b j -> p (b j)").bitcast(F32)
+            x_grouped[c] = two.tile([P, CHUNK, PACK], BF16, name="x_grouped", align_bytes=64)
+            x_grouped_words = x_grouped[c][:].rearrange("p b j -> p (b j)").bitcast(F32)
             words = FEATURES // 2
             for pair in range(2):
                 x_t = psum_x.tile([P, 2, CHUNK // 2], F32, name="x_t")
@@ -139,51 +152,109 @@ def tile_infovae_pa_t_kernel(
                     ),
                     in_=x_t[:].rearrange("p u b -> p b u"),
                 )
-            return x_grouped
+
+        def quantise_x(c):
+            if live(c):
+                x_q[c] = quantise(nc, three, x_grouped[c], "x")
 
         def hidden(c):
-            y_mu = work.tile([P, HIDDEN_TILES, CHUNK], F32, name="y_mu")
-            h_sig = work.tile([P, HIDDEN_TILES, CHUNK], BF16, name="h_sig")
+            if not live(c):
+                return
+            y_mu[c] = two.tile([P, HIDDEN_TILES, CHUNK], F32, name="y_mu")
+            h_sig[c] = two.tile([P, HIDDEN_TILES, CHUNK], BF16, name="h_sig")
             for m in range(HIDDEN_TILES):
                 acc = psum_h.tile([P, CHUNK], F32, name="acc")
                 mx_pass(nc, acc, w1_mu_q, slice(m * P, (m + 1) * P), x_q[c])
                 nc.scalar.activation(
-                    out=y_mu[:, m, :], in_=acc[:], func=ACT.Identity, bias=b1_mu_f[:, m : m + 1], scale=1.0
+                    out=y_mu[c][:, m, :], in_=acc[:], func=ACT.Identity, bias=b1_mu_f[:, m : m + 1], scale=1.0
                 )
             for m in range(HIDDEN_TILES):
                 acc = psum_h.tile([P, CHUNK], F32, name="acc")
                 mx_pass(nc, acc, w1_sig_q, slice(m * P, (m + 1) * P), x_q[c])
                 nc.scalar.activation(
-                    out=h_sig[:, m, :], in_=acc[:], func=ACT.Tanh, bias=b1_sig_f[:, m : m + 1], scale=1.0
+                    out=h_sig[c][:, m, :], in_=acc[:], func=ACT.Tanh, bias=b1_sig_f[:, m : m + 1], scale=1.0
                 )
-            return y_mu, h_sig
 
-        def output_layers(c):
-            y_out = work.tile([P, 2, CHUNK], F32, name="y_out")
-            for s, (w, h, b) in enumerate(((w2_mu_q, h_mu_q[c], b2_mu_f), (w2_sig_q, h_sig_q[c], b2_sig_f))):
-                acc = psum_o.tile([P, CHUNK], F32, name="acc_o")
-                mx_pass(nc, acc, w, slice(0, LATENT), h)
-                nc.scalar.activation(out=y_out[:, s, :], in_=acc[:], func=ACT.Identity, bias=b[:, 0:1], scale=1.0)
-            return y_out
+        def group_h_mu(c):
+            if live(c):
+                h_mu_grouped[c] = two.tile([P, CHUNK, PACK], BF16, name="h_mu_grouped", align_bytes=64)
+                leaky(nc, h_mu_grouped[c][:], y_mu[c][:].rearrange("p m b -> p b m"))
 
-        def samples(c):
-            mean = psum_o.tile([P, CHUNK], F32, name="mean")
-            std = psum_o.tile([P, CHUNK], F32, name="std")
-            for back, turned in ((std, std_t[c]), (mean, mean_t[c])):
+        def group_h_sig_scalar(c):
+            if live(c):
+                h_sig_grouped[c] = two.tile([P, CHUNK, PACK], BF16, name="h_sig_grouped", align_bytes=64)
+                to_s, from_s = side_by_side(h_sig[c], h_sig_grouped[c], slice(0, SCALAR_COLS))
+                nc.scalar.copy(out=to_s, in_=from_s)
+
+        def group_h_sig_vector(c):
+            if live(c):
+                to_v, from_v = side_by_side(h_sig[c], h_sig_grouped[c], slice(SCALAR_COLS, CHUNK))
+                nc.vector.tensor_copy(out=to_v, in_=from_v)
+
+        def quantise_h_mu(c):
+            if live(c):
+                h_mu_q[c] = quantise(nc, two, h_mu_grouped[c], "h_mu")
+
+        def quantise_h_sig(c):
+            if live(c):
+                h_sig_q[c] = quantise(nc, two, h_sig_grouped[c], "h_sig")
+
+        def output_layer(c, s, w, h_q, b):
+            if not live(c):
+                return
+            if s == 0:
+                y_out[c] = two.tile([P, 2, CHUNK], F32, name="y_out")
+            acc = psum_o.tile([P, CHUNK], F32, name="acc_o")
+            mx_pass(nc, acc, w, slice(0, LATENT), h_q[c])
+            nc.scalar.activation(out=y_out[c][:, s, :], in_=acc[:], func=ACT.Identity, bias=b[:, 0:1], scale=1.0)
+
+        def leaky_out(c):
+            if live(c):
+                l_out[c] = two.tile([P, 2, CHUNK], F32, name="l_out")
+                leaky(nc, l_out[c][:], y_out[c][:])
+
+        def clip_log_var(c):
+            if live(c):
+                lv_clipped[c] = two.tile([P, CHUNK], F32, name="lv_clipped")
+                nc.vector.tensor_scalar(
+                    out=lv_clipped[c][:], in0=l_out[c][:, 1, :], scalar1=LV_MAX, scalar2=LV_MIN,
+                    op0=ALU.min, op1=ALU.max,
+                )
+
+        def std_dev(c):
+            if live(c):
+                std_t[c] = two.tile([P, CHUNK], F32, name="std_t")
+                nc.scalar.activation(out=std_t[c][:], in_=lv_clipped[c][:], func=ACT.Exp, scale=0.5)
+
+        def turn_back(c):
+            if not live(c):
+                return
+            std[c] = psum_o.tile([P, CHUNK], F32, name="std")
+            mean[c] = psum_o.tile([P, CHUNK], F32, name="mean")
+            for back, turned in ((std[c], std_t[c]), (mean[c], l_out[c][:, 0, :])):
                 for t in range(ROW_TILES):
                     cols = slice(t * P, (t + 1) * P)
                     nc.tensor.transpose(back[:, cols], turned[:, cols], identity[:])
-            z = work.tile([P, 2, CHUNK], F32, name="z")
-            nc.vector.tensor_tensor(
-                out=z[:], in0=std[:].unsqueeze(1).to_broadcast([P, 2, CHUNK]), in1=noise[c][:], op=ALU.mult
-            )
-            nc.vector.tensor_tensor(
-                out=z[:], in0=z[:], in1=mean[:].unsqueeze(1).to_broadcast([P, 2, CHUNK]), op=ALU.add
-            )
-            for s in range(2):
-                nc.sync.dma_start(out=out_chunks[s][c], in_=z[:, s, :])
 
-        load(0)
+        def scale_noise(c):
+            if live(c):
+                z[c] = three.tile([P, 2, CHUNK], F32, name="z")
+                nc.vector.tensor_tensor(
+                    out=z[c][:], in0=std[c][:].unsqueeze(1).to_broadcast([P, 2, CHUNK]), in1=noise[c][:],
+                    op=ALU.mult,
+                )
+
+        def add_mean(c):
+            if live(c):
+                nc.vector.tensor_tensor(
+                    out=z[c][:], in0=z[c][:], in1=mean[c][:].unsqueeze(1).to_broadcast([P, 2, CHUNK]),
+                    op=ALU.add,
+                )
+                for s in range(2):
+                    nc.sync.dma_start(out=out_chunks[s][c], in_=z[c][:, s, :])
+
+
+        load_x(0)
         identity = keep.tile([P, P], F32, name="identity")
         make_identity(nc, identity[:])
         zero = keep.tile([P, 1], F32, name="zero")
@@ -193,40 +264,36 @@ def tile_infovae_pa_t_kernel(
 
         w1_mu_q = quantise_weight(nc, stage, keep, w1_mu, HIDDEN, "w1_mu", True)
         b1_mu_f = load_bias(nc, stage, keep, b1_mu, HIDDEN_TILES, "b1_mu")
+        turn_x(0)
+        quantise_x(0)
         w1_sig_q = quantise_weight(nc, stage, keep, w1_sig, HIDDEN, "w1_sig", True)
         b1_sig_f = load_bias(nc, stage, keep, b1_sig, HIDDEN_TILES, "b1_sig")
-        load(1)
+        load_x(1)
+        load_x(2)
         w2_mu_q = quantise_weight(nc, stage, keep, w2_mu, LATENT, "w2_mu", False)
         b2_mu_f = load_bias(nc, stage, keep, b2_mu, 1, "b2_mu")
         w2_sig_q = quantise_weight(nc, stage, keep, w2_sig, LATENT, "w2_sig", False)
         b2_sig_f = load_bias(nc, stage, keep, b2_sig, 1, "b2_sig")
+        load_noise(0)
+        turn_x(1)
+        quantise_x(1)
 
-        for c in range(N_CHUNKS):
-            if c + 2 < N_CHUNKS:
-                load(c + 2)
-            x_grouped = transpose_x(c)
-            x_q[c] = quantise(nc, work, x_grouped, "x")
-
-            y_mu, h_sig = hidden(c)
-            h_mu_grouped = work.tile([P, CHUNK, PACK], BF16, name="h_mu_grouped", align_bytes=64)
-            leaky(nc, h_mu_grouped[:], y_mu[:].rearrange("p m b -> p b m"))
-            h_sig_grouped = work.tile([P, CHUNK, PACK], BF16, name="h_sig_grouped", align_bytes=64)
-            to_s, from_s = side_by_side(h_sig, h_sig_grouped, slice(0, SCALAR_COLS))
-            nc.scalar.copy(out=to_s, in_=from_s)
-            to_v, from_v = side_by_side(h_sig, h_sig_grouped, slice(SCALAR_COLS, CHUNK))
-            nc.vector.tensor_copy(out=to_v, in_=from_v)
-            h_mu_q[c] = quantise(nc, work, h_mu_grouped, "h_mu")
-            h_sig_q[c] = quantise(nc, work, h_sig_grouped, "h_sig")
-
-            y_out = output_layers(c)
-            l_out = work.tile([P, 2, CHUNK], F32, name="l_out")
-            leaky(nc, l_out[:], y_out[:])
-            mean_t[c] = l_out[:, 0, :]
-            lv_clipped[c] = work.tile([P, CHUNK], F32, name="lv_clipped")
-            nc.vector.tensor_scalar(
-                out=lv_clipped[c][:], in0=l_out[:, 1, :], scalar1=LV_MAX, scalar2=LV_MIN,
-                op0=ALU.min, op1=ALU.max,
-            )
-            std_t[c] = work.tile([P, CHUNK], F32, name="std_t")
-            nc.scalar.activation(out=std_t[c][:], in_=lv_clipped[c][:], func=ACT.Exp, scale=0.5)
-            samples(c)
+        for i in range(N_CHUNKS + 3):
+            load_x(i + 3)
+            load_noise(i + 1)
+            hidden(i)
+            turn_x(i + 2)
+            output_layer(i - 1, 0, w2_mu_q, h_mu_q, b2_mu_f)
+            turn_back(i - 3)
+            group_h_sig_scalar(i)
+            output_layer(i - 1, 1, w2_sig_q, h_sig_q, b2_sig_f)
+            group_h_mu(i)
+            leaky_out(i - 2)
+            group_h_sig_vector(i)
+            clip_log_var(i - 2)
+            std_dev(i - 2)
+            quantise_h_mu(i)
+            scale_noise(i - 3)
+            quantise_h_sig(i)
+            add_mean(i - 3)
+            quantise_x(i + 2)

@@ -21,7 +21,7 @@ HIDDEN_TILES = HIDDEN // P
 NEG_SLOPE = 0.01
 LV_MIN, LV_MAX = -10.0, 10.0
 
-SCALAR_COLS = 192
+SCALAR_COLS = 320
 
 FLOPS = 2 * BATCH * 2 * (FEATURES * HIDDEN + HIDDEN * LATENT)
 

@@ -1,3 +1,4 @@
+import math
 from contextlib import ExitStack
 
 import concourse.mybir as mybir
@@ -20,8 +21,9 @@ N_CHUNKS = BATCH // CHUNK
 HIDDEN_TILES = HIDDEN // P
 NEG_SLOPE = 0.01
 LV_MIN, LV_MAX = -10.0, 10.0
+STD_MIN, STD_MAX = math.exp(0.5 * LV_MIN), math.exp(0.5 * LV_MAX)
 
-SCALAR_COLS = 320
+SCALAR_COLS = 272
 
 FLOPS = 2 * BATCH * 2 * (FEATURES * HIDDEN + HIDDEN * LATENT)
 
@@ -112,7 +114,7 @@ def tile_infovae_pa_t_kernel(
 
         x_rows, noise, x_grouped, x_q, y_mu, h_sig = {}, {}, {}, {}, {}, {}
         h_mu_grouped, h_sig_grouped, h_mu_q, h_sig_q = {}, {}, {}, {}
-        y_out, l_out, lv_clipped, std_t, mean, std, z = {}, {}, {}, {}, {}, {}, {}
+        y_out, l_out, e_steep, e_flat, std_t, mean, std, z = {}, {}, {}, {}, {}, {}, {}, {}
 
         def live(c):
             return 0 <= c < N_CHUNKS
@@ -199,39 +201,49 @@ def tile_infovae_pa_t_kernel(
             if live(c):
                 h_sig_q[c] = quantise(nc, two, h_sig_grouped[c], "h_sig")
 
-        def output_layer(c, s, w, h_q, b):
+        def output_mean(c):
             if not live(c):
                 return
-            if s == 0:
-                y_out[c] = two.tile([P, 2, CHUNK], F32, name="y_out")
+            y_out[c] = two.tile([P, CHUNK], F32, name="y_out")
             acc = psum_o.tile([P, CHUNK], F32, name="acc_o")
-            mx_pass(nc, acc, w, slice(0, LATENT), h_q[c])
-            nc.scalar.activation(out=y_out[c][:, s, :], in_=acc[:], func=ACT.Identity, bias=b[:, 0:1], scale=1.0)
+            mx_pass(nc, acc, w2_mu_q, slice(0, LATENT), h_mu_q[c])
+            nc.scalar.activation(
+                out=y_out[c][:], in_=acc[:], func=ACT.Identity, bias=b2_mu_f[:, 0:1], scale=1.0
+            )
 
-        def leaky_out(c):
+        def output_std(c):
+            if not live(c):
+                return
+            e_steep[c] = two.tile([P, CHUNK], F32, name="e_steep")
+            e_flat[c] = two.tile([P, CHUNK], F32, name="e_flat")
+            acc = psum_o.tile([P, CHUNK], F32, name="acc_o")
+            mx_pass(nc, acc, w2_sig_q, slice(0, LATENT), h_sig_q[c])
+            nc.scalar.activation(
+                out=e_steep[c][:], in_=acc[:], func=ACT.Exp, bias=b2_sig_steep[:, 0:1], scale=0.5
+            )
+            nc.scalar.activation(
+                out=e_flat[c][:], in_=acc[:], func=ACT.Exp, bias=b2_sig_flat[:, 0:1], scale=0.5 * NEG_SLOPE
+            )
+
+        def leaky_mean(c):
             if live(c):
-                l_out[c] = two.tile([P, 2, CHUNK], F32, name="l_out")
+                l_out[c] = two.tile([P, CHUNK], F32, name="l_out")
                 leaky(nc, l_out[c][:], y_out[c][:])
-
-        def clip_log_var(c):
-            if live(c):
-                lv_clipped[c] = two.tile([P, CHUNK], F32, name="lv_clipped")
-                nc.vector.tensor_scalar(
-                    out=lv_clipped[c][:], in0=l_out[c][:, 1, :], scalar1=LV_MAX, scalar2=LV_MIN,
-                    op0=ALU.min, op1=ALU.max,
-                )
 
         def std_dev(c):
             if live(c):
                 std_t[c] = two.tile([P, CHUNK], F32, name="std_t")
-                nc.scalar.activation(out=std_t[c][:], in_=lv_clipped[c][:], func=ACT.Exp, scale=0.5)
+                nc.vector.scalar_tensor_tensor(
+                    out=std_t[c][:], in0=e_steep[c][:], scalar=STD_MIN, in1=e_flat[c][:],
+                    op0=ALU.max, op1=ALU.max,
+                )
 
         def turn_back(c):
             if not live(c):
                 return
             std[c] = psum_o.tile([P, CHUNK], F32, name="std")
             mean[c] = psum_o.tile([P, CHUNK], F32, name="mean")
-            for back, turned in ((std[c], std_t[c]), (mean[c], l_out[c][:, 0, :])):
+            for back, turned in ((std[c], std_t[c]), (mean[c], l_out[c])):
                 for t in range(ROW_TILES):
                     cols = slice(t * P, (t + 1) * P)
                     nc.tensor.transpose(back[:, cols], turned[:, cols], identity[:])
@@ -239,9 +251,9 @@ def tile_infovae_pa_t_kernel(
         def scale_noise(c):
             if live(c):
                 z[c] = three.tile([P, 2, CHUNK], F32, name="z")
-                nc.vector.tensor_tensor(
-                    out=z[c][:], in0=std[c][:].unsqueeze(1).to_broadcast([P, 2, CHUNK]), in1=noise[c][:],
-                    op=ALU.mult,
+                nc.vector.scalar_tensor_tensor(
+                    out=z[c][:], in0=std[c][:].unsqueeze(1).to_broadcast([P, 2, CHUNK]), scalar=STD_MAX,
+                    in1=noise[c][:], op0=ALU.min, op1=ALU.mult,
                 )
 
         def add_mean(c):
@@ -274,6 +286,12 @@ def tile_infovae_pa_t_kernel(
         b2_mu_f = load_bias(nc, stage, keep, b2_mu, 1, "b2_mu")
         w2_sig_q = quantise_weight(nc, stage, keep, w2_sig, LATENT, "w2_sig", False)
         b2_sig_f = load_bias(nc, stage, keep, b2_sig, 1, "b2_sig")
+        b2_sig_steep = keep.tile([P, 1], F32, name="b2_sig_steep")
+        nc.vector.tensor_scalar(out=b2_sig_steep[:], in0=b2_sig_f[:], scalar1=0.5, scalar2=None, op0=ALU.mult)
+        b2_sig_flat = keep.tile([P, 1], F32, name="b2_sig_flat")
+        nc.vector.tensor_scalar(
+            out=b2_sig_flat[:], in0=b2_sig_f[:], scalar1=0.5 * NEG_SLOPE, scalar2=None, op0=ALU.mult
+        )
         load_noise(0)
         turn_x(1)
         quantise_x(1)
@@ -283,14 +301,13 @@ def tile_infovae_pa_t_kernel(
             load_noise(i + 1)
             hidden(i)
             turn_x(i + 2)
-            output_layer(i - 1, 0, w2_mu_q, h_mu_q, b2_mu_f)
+            output_mean(i - 1)
             turn_back(i - 3)
             group_h_sig_scalar(i)
-            output_layer(i - 1, 1, w2_sig_q, h_sig_q, b2_sig_f)
+            output_std(i - 1)
             group_h_mu(i)
-            leaky_out(i - 2)
+            leaky_mean(i - 2)
             group_h_sig_vector(i)
-            clip_log_var(i - 2)
             std_dev(i - 2)
             quantise_h_mu(i)
             scale_noise(i - 3)

@@ -23,8 +23,6 @@ NEG_SLOPE = 0.01
 LV_MIN, LV_MAX = -10.0, 10.0
 STD_MIN, STD_MAX = math.exp(0.5 * LV_MIN), math.exp(0.5 * LV_MAX)
 
-SCALAR_COLS = 272
-
 FLOPS = 2 * BATCH * 2 * (FEATURES * HIDDEN + HIDDEN * LATENT)
 
 
@@ -84,13 +82,6 @@ def leaky(nc, out, y):
     nc.vector.scalar_tensor_tensor(out=out, in0=y, scalar=NEG_SLOPE, in1=y, op0=ALU.mult, op1=ALU.max)
 
 
-def side_by_side(planes, grouped, cols):
-    return (
-        grouped[:, cols, :].rearrange("p (c i) j -> p c j i", i=4),
-        planes[:, :, cols].rearrange("p j (c i) -> p c j i", i=4),
-    )
-
-
 def tile_infovae_pa_t_kernel(
     tc, x, noise_enc, noise_z, w1_mu, b1_mu, w2_mu, b2_mu, w1_sig, b1_sig, w2_sig, b2_sig, out_0, out_1
 ):
@@ -104,17 +95,18 @@ def tile_infovae_pa_t_kernel(
     with ExitStack() as ctx:
         keep = ctx.enter_context(tc.tile_pool(name="keep", bufs=1))
         stage = ctx.enter_context(tc.tile_pool(name="stage", bufs=1))
+        one = ctx.enter_context(tc.tile_pool(name="one", bufs=1))
         two = ctx.enter_context(tc.tile_pool(name="two", bufs=2))
         three = ctx.enter_context(tc.tile_pool(name="three", bufs=3))
         six = ctx.enter_context(tc.tile_pool(name="six", bufs=6))
-        psum_x = ctx.enter_context(tc.psum_pool(name="psum_x", bufs=2))
+        psum_x = ctx.enter_context(tc.psum_pool(name="psum_x", bufs=1))
         psum_h = ctx.enter_context(tc.psum_pool(name="psum_h", bufs=3))
         psum_o = ctx.enter_context(tc.psum_pool(name="psum_o", bufs=1))
         ctx.enter_context(tc.manual_schedule())
 
         x_rows, noise, x_grouped, x_q, y_mu, h_sig = {}, {}, {}, {}, {}, {}
         h_mu_grouped, h_sig_grouped, h_mu_q, h_sig_q = {}, {}, {}, {}
-        y_out, l_out, e_steep, e_flat, std_t, mean, std, z = {}, {}, {}, {}, {}, {}, {}, {}
+        acc_mean, flat, l_out, e_steep, e_flat, std_t, mean, std, z = {}, {}, {}, {}, {}, {}, {}, {}, {}
 
         def live(c):
             return 0 <= c < N_CHUNKS
@@ -131,29 +123,27 @@ def tile_infovae_pa_t_kernel(
                 for s in range(2):
                     nc.sync.dma_start(out=noise[c][:, s, :], in_=noise_chunks[s][c])
 
-        def turn_x(c):
+        def turn_x(c, pair):
             if not live(c):
                 return
             x_words = x_rows[c][:].bitcast(F32)
-            x_grouped[c] = two.tile([P, CHUNK, PACK], BF16, name="x_grouped", align_bytes=64)
+            if pair == 0:
+                x_grouped[c] = two.tile([P, CHUNK, PACK], BF16, name="x_grouped", align_bytes=64)
             x_grouped_words = x_grouped[c][:].rearrange("p b j -> p (b j)").bitcast(F32)
             words = FEATURES // 2
-            for pair in range(2):
-                x_t = psum_x.tile([P, 2, CHUNK // 2], F32, name="x_t")
-                for tt in range(2):
-                    t = 2 * pair + tt
-                    for u in range(2):
-                        nc.tensor.transpose(
-                            x_t[:, u, tt * P : (tt + 1) * P],
-                            x_words[:, t * words + u : (t + 1) * words : 2],
-                            identity[:],
-                        )
-                nc.scalar.copy(
-                    out=x_grouped_words[:, pair * CHUNK : (pair + 1) * CHUNK].rearrange(
-                        "p (b u) -> p b u", u=2
-                    ),
-                    in_=x_t[:].rearrange("p u b -> p b u"),
-                )
+            x_t = psum_x.tile([P, 2, CHUNK // 2], F32, name="x_t")
+            for tt in range(2):
+                t = 2 * pair + tt
+                for u in range(2):
+                    nc.tensor.transpose(
+                        x_t[:, u, tt * P : (tt + 1) * P],
+                        x_words[:, t * words + u : (t + 1) * words : 2],
+                        identity[:],
+                    )
+            nc.scalar.copy(
+                out=x_grouped_words[:, pair * CHUNK : (pair + 1) * CHUNK].rearrange("p (b u) -> p b u", u=2),
+                in_=x_t[:].rearrange("p u b -> p b u"),
+            )
 
         def quantise_x(c):
             if live(c):
@@ -182,16 +172,13 @@ def tile_infovae_pa_t_kernel(
                 h_mu_grouped[c] = two.tile([P, CHUNK, PACK], BF16, name="h_mu_grouped", align_bytes=64)
                 leaky(nc, h_mu_grouped[c][:], y_mu[c][:].rearrange("p m b -> p b m"))
 
-        def group_h_sig_scalar(c):
+        def group_h_sig(c):
             if live(c):
-                h_sig_grouped[c] = two.tile([P, CHUNK, PACK], BF16, name="h_sig_grouped", align_bytes=64)
-                to_s, from_s = side_by_side(h_sig[c], h_sig_grouped[c], slice(0, SCALAR_COLS))
-                nc.scalar.copy(out=to_s, in_=from_s)
-
-        def group_h_sig_vector(c):
-            if live(c):
-                to_v, from_v = side_by_side(h_sig[c], h_sig_grouped[c], slice(SCALAR_COLS, CHUNK))
-                nc.vector.tensor_copy(out=to_v, in_=from_v)
+                h_sig_grouped[c] = one.tile([P, CHUNK, PACK], BF16, name="h_sig_grouped", align_bytes=64)
+                nc.gpsimd.tensor_scalar(
+                    out=h_sig_grouped[c][:], in0=h_sig[c][:].rearrange("p m b -> p b m"),
+                    scalar1=1.0, scalar2=0.0, op0=ALU.mult, op1=ALU.add,
+                )
 
         def quantise_h_mu(c):
             if live(c):
@@ -204,11 +191,11 @@ def tile_infovae_pa_t_kernel(
         def output_mean(c):
             if not live(c):
                 return
-            y_out[c] = two.tile([P, CHUNK], F32, name="y_out")
-            acc = psum_o.tile([P, CHUNK], F32, name="acc_o")
-            mx_pass(nc, acc, w2_mu_q, slice(0, LATENT), h_mu_q[c])
+            acc_mean[c] = psum_o.tile([P, CHUNK], F32, name="acc_mean")
+            mx_pass(nc, acc_mean[c], w2_mu_q, slice(0, LATENT), h_mu_q[c])
+            flat[c] = two.tile([P, CHUNK], F32, name="flat")
             nc.scalar.activation(
-                out=y_out[c][:], in_=acc[:], func=ACT.Identity, bias=b2_mu_f[:, 0:1], scale=1.0
+                out=flat[c][:], in_=acc_mean[c][:], func=ACT.Identity, bias=b2_mu_flat[:, 0:1], scale=NEG_SLOPE
             )
 
         def output_std(c):
@@ -216,7 +203,7 @@ def tile_infovae_pa_t_kernel(
                 return
             e_steep[c] = two.tile([P, CHUNK], F32, name="e_steep")
             e_flat[c] = two.tile([P, CHUNK], F32, name="e_flat")
-            acc = psum_o.tile([P, CHUNK], F32, name="acc_o")
+            acc = psum_o.tile([P, CHUNK], F32, name="acc_std")
             mx_pass(nc, acc, w2_sig_q, slice(0, LATENT), h_sig_q[c])
             nc.scalar.activation(
                 out=e_steep[c][:], in_=acc[:], func=ACT.Exp, bias=b2_sig_steep[:, 0:1], scale=0.5
@@ -228,7 +215,10 @@ def tile_infovae_pa_t_kernel(
         def leaky_mean(c):
             if live(c):
                 l_out[c] = two.tile([P, CHUNK], F32, name="l_out")
-                leaky(nc, l_out[c][:], y_out[c][:])
+                nc.vector.scalar_tensor_tensor(
+                    out=l_out[c][:], in0=acc_mean[c][:], scalar=b2_mu_f[:, 0:1], in1=flat[c][:],
+                    op0=ALU.add, op1=ALU.max,
+                )
 
         def std_dev(c):
             if live(c):
@@ -276,7 +266,8 @@ def tile_infovae_pa_t_kernel(
 
         w1_mu_q = quantise_weight(nc, stage, keep, w1_mu, HIDDEN, "w1_mu", True)
         b1_mu_f = load_bias(nc, stage, keep, b1_mu, HIDDEN_TILES, "b1_mu")
-        turn_x(0)
+        turn_x(0, 0)
+        turn_x(0, 1)
         quantise_x(0)
         w1_sig_q = quantise_weight(nc, stage, keep, w1_sig, HIDDEN, "w1_sig", True)
         b1_sig_f = load_bias(nc, stage, keep, b1_sig, HIDDEN_TILES, "b1_sig")
@@ -284,6 +275,8 @@ def tile_infovae_pa_t_kernel(
         load_x(2)
         w2_mu_q = quantise_weight(nc, stage, keep, w2_mu, LATENT, "w2_mu", False)
         b2_mu_f = load_bias(nc, stage, keep, b2_mu, 1, "b2_mu")
+        b2_mu_flat = keep.tile([P, 1], F32, name="b2_mu_flat")
+        nc.vector.tensor_scalar(out=b2_mu_flat[:], in0=b2_mu_f[:], scalar1=NEG_SLOPE, scalar2=None, op0=ALU.mult)
         w2_sig_q = quantise_weight(nc, stage, keep, w2_sig, LATENT, "w2_sig", False)
         b2_sig_f = load_bias(nc, stage, keep, b2_sig, 1, "b2_sig")
         b2_sig_steep = keep.tile([P, 1], F32, name="b2_sig_steep")
@@ -293,24 +286,24 @@ def tile_infovae_pa_t_kernel(
             out=b2_sig_flat[:], in0=b2_sig_f[:], scalar1=0.5 * NEG_SLOPE, scalar2=None, op0=ALU.mult
         )
         load_noise(0)
-        turn_x(1)
-        quantise_x(1)
+        turn_x(1, 0)
+        turn_x(1, 1)
 
         for i in range(N_CHUNKS + 3):
             load_x(i + 3)
             load_noise(i + 1)
             hidden(i)
-            turn_x(i + 2)
+            turn_x(i + 2, 0)
             output_mean(i - 1)
+            output_std(i - 2)
             turn_back(i - 3)
-            group_h_sig_scalar(i)
-            output_std(i - 1)
+            turn_x(i + 2, 1)
             group_h_mu(i)
-            leaky_mean(i - 2)
-            group_h_sig_vector(i)
-            std_dev(i - 2)
+            quantise_x(i + 1)
             quantise_h_mu(i)
+            quantise_h_sig(i - 1)
+            group_h_sig(i)
             scale_noise(i - 3)
-            quantise_h_sig(i)
+            leaky_mean(i - 1)
             add_mean(i - 3)
-            quantise_x(i + 2)
+            std_dev(i - 2)

@@ -23,6 +23,8 @@ NEG_SLOPE = 0.01
 LV_MIN, LV_MAX = -10.0, 10.0
 STD_MIN, STD_MAX = math.exp(0.5 * LV_MIN), math.exp(0.5 * LV_MAX)
 
+GPSIMD_COLS = 384
+
 FLOPS = 2 * BATCH * 2 * (FEATURES * HIDDEN + HIDDEN * LATENT)
 
 
@@ -176,8 +178,13 @@ def tile_infovae_pa_t_kernel(
             if live(c):
                 h_sig_grouped[c] = one.tile([P, CHUNK, PACK], BF16, name="h_sig_grouped", align_bytes=64)
                 nc.gpsimd.tensor_scalar(
-                    out=h_sig_grouped[c][:], in0=h_sig[c][:].rearrange("p m b -> p b m"),
+                    out=h_sig_grouped[c][:, 0:GPSIMD_COLS, :],
+                    in0=h_sig[c][:, :, 0:GPSIMD_COLS].rearrange("p m b -> p b m"),
                     scalar1=1.0, scalar2=0.0, op0=ALU.mult, op1=ALU.add,
+                )
+                nc.scalar.copy(
+                    out=h_sig_grouped[c][:, GPSIMD_COLS:CHUNK, :].rearrange("p (c i) j -> p c j i", i=4),
+                    in_=h_sig[c][:, :, GPSIMD_COLS:CHUNK].rearrange("p j (c i) -> p c j i", i=4),
                 )
 
         def quantise_h_mu(c):

@@ -151,17 +151,21 @@ def tile_infovae_pa_t_kernel(
             if live(c):
                 x_q[c] = quantise(nc, three, x_grouped[c], "x")
 
-        def hidden(c):
+        def hidden_mu(c):
             if not live(c):
                 return
             y_mu[c] = two.tile([P, HIDDEN_TILES, CHUNK], F32, name="y_mu")
-            h_sig[c] = two.tile([P, HIDDEN_TILES, CHUNK], BF16, name="h_sig")
             for m in range(HIDDEN_TILES):
                 acc = psum_h.tile([P, CHUNK], F32, name="acc")
                 mx_pass(nc, acc, w1_mu_q, slice(m * P, (m + 1) * P), x_q[c])
                 nc.scalar.activation(
                     out=y_mu[c][:, m, :], in_=acc[:], func=ACT.Identity, bias=b1_mu_f[:, m : m + 1], scale=1.0
                 )
+
+        def hidden_sig(c):
+            if not live(c):
+                return
+            h_sig[c] = two.tile([P, HIDDEN_TILES, CHUNK], BF16, name="h_sig")
             for m in range(HIDDEN_TILES):
                 acc = psum_h.tile([P, CHUNK], F32, name="acc")
                 mx_pass(nc, acc, w1_sig_q, slice(m * P, (m + 1) * P), x_q[c])
@@ -295,22 +299,24 @@ def tile_infovae_pa_t_kernel(
         load_noise(0)
         turn_x(1, 0)
         turn_x(1, 1)
+        quantise_x(1)
 
-        for i in range(N_CHUNKS + 3):
+        for i in range(N_CHUNKS + 2):
             load_x(i + 3)
             load_noise(i + 1)
-            hidden(i)
-            turn_x(i + 2, 0)
+            hidden_mu(i)
+            hidden_sig(i)
             output_mean(i - 1)
-            output_std(i - 2)
-            turn_back(i - 3)
+            group_h_sig(i)
+            turn_back(i - 2)
+            turn_x(i + 2, 0)
+            output_std(i - 1)
             turn_x(i + 2, 1)
             group_h_mu(i)
-            quantise_x(i + 1)
-            quantise_h_mu(i)
-            quantise_h_sig(i - 1)
-            group_h_sig(i)
-            scale_noise(i - 3)
+            scale_noise(i - 2)
             leaky_mean(i - 1)
-            add_mean(i - 3)
-            std_dev(i - 2)
+            add_mean(i - 2)
+            quantise_h_mu(i)
+            std_dev(i - 1)
+            quantise_x(i + 2)
+            quantise_h_sig(i)

@@ -28,9 +28,14 @@ GPSIMD_COLS = 384
 FLOPS = 2 * BATCH * 2 * (FEATURES * HIDDEN + HIDDEN * LATENT)
 
 
-def quantise_weight(nc, stage, keep, w, cols, name, spread):
+def load_weight(nc, stage, w, cols, name):
     raw = stage.tile([P, PACK, cols], BF16, name=name + "_raw")
     nc.sync.dma_start(out=raw[:], in_=w.rearrange("(p j) n -> p j n", j=PACK))
+    return raw
+
+
+def group_weight(nc, stage, raw, name, spread):
+    cols = raw.shape[2]
     grouped = stage.tile([P, cols, PACK], BF16, name=name + "_grouped", align_bytes=64)
     if spread:
         nc.vector.tensor_copy(
@@ -39,6 +44,11 @@ def quantise_weight(nc, stage, keep, w, cols, name, spread):
         )
     else:
         nc.vector.tensor_copy(out=grouped[:], in_=raw[:].rearrange("p j n -> p n j"))
+    return grouped
+
+
+def quantise_weight(nc, keep, grouped, name):
+    cols = grouped.shape[1]
     codes = keep.tile([P, cols], U32, name=name + "_codes", align_bytes=64)
     scales = keep.tile([P, cols], U8, name=name + "_scales", align_bytes=64)
     nc.vector.quantize_mx(
@@ -49,11 +59,15 @@ def quantise_weight(nc, stage, keep, w, cols, name, spread):
     return codes, scales
 
 
-def load_bias(nc, stage, keep, b, per_partition, name):
+def load_bias(nc, stage, b, per_partition, name):
     raw = stage.tile([P, per_partition], BF16, name=name + "_raw")
     nc.sync.dma_start(out=raw[:], in_=b.rearrange("(p m) -> p m", m=per_partition))
-    bias = keep.tile([P, per_partition], F32, name=name)
-    nc.vector.tensor_copy(out=bias[:], in_=raw[:])
+    return raw
+
+
+def scaled_bias(nc, keep, raw, scale, name):
+    bias = keep.tile([P, raw.shape[1]], F32, name=name)
+    nc.vector.tensor_scalar(out=bias[:], in0=raw[:], scalar1=scale, scalar2=None, op0=ALU.mult)
     return bias
 
 
@@ -82,6 +96,13 @@ def mx_pass(nc, acc, weight, w_cols, moving):
 
 def leaky(nc, out, y):
     nc.vector.scalar_tensor_tensor(out=out, in0=y, scalar=NEG_SLOPE, in1=y, op0=ALU.mult, op1=ALU.max)
+
+
+def side_by_side(planes, grouped, cols):
+    return (
+        grouped[:, cols, :].rearrange("p (c i) j -> p c j i", i=4),
+        planes[:, :, cols].rearrange("p j (c i) -> p c j i", i=4),
+    )
 
 
 def tile_infovae_pa_t_kernel(
@@ -114,10 +135,13 @@ def tile_infovae_pa_t_kernel(
             return 0 <= c < N_CHUNKS
 
 
-        def load_x(c):
+        def load_x(c, parts=1):
             if live(c):
                 x_rows[c] = three.tile([P, ROW_TILES * FEATURES], BF16, name="x_rows")
-                nc.sync.dma_start(out=x_rows[c][:], in_=x_chunks[c])
+                width = ROW_TILES * FEATURES // parts
+                for k in range(parts):
+                    part = slice(k * width, (k + 1) * width)
+                    nc.sync.dma_start(out=x_rows[c][:, part], in_=x_chunks[c][:, part])
 
         def load_noise(c):
             if live(c):
@@ -125,7 +149,7 @@ def tile_infovae_pa_t_kernel(
                 for s in range(2):
                     nc.sync.dma_start(out=noise[c][:, s, :], in_=noise_chunks[s][c])
 
-        def turn_x(c, pair):
+        def turn_x(c, pair, pool=psum_x, bank="x_t", copy=nc.scalar.copy):
             if not live(c):
                 return
             x_words = x_rows[c][:].bitcast(F32)
@@ -133,7 +157,7 @@ def tile_infovae_pa_t_kernel(
                 x_grouped[c] = two.tile([P, CHUNK, PACK], BF16, name="x_grouped", align_bytes=64)
             x_grouped_words = x_grouped[c][:].rearrange("p b j -> p (b j)").bitcast(F32)
             words = FEATURES // 2
-            x_t = psum_x.tile([P, 2, CHUNK // 2], F32, name="x_t")
+            x_t = pool.tile([P, 2, CHUNK // 2], F32, name=bank)
             for tt in range(2):
                 t = 2 * pair + tt
                 for u in range(2):
@@ -142,7 +166,7 @@ def tile_infovae_pa_t_kernel(
                         x_words[:, t * words + u : (t + 1) * words : 2],
                         identity[:],
                     )
-            nc.scalar.copy(
+            copy(
                 out=x_grouped_words[:, pair * CHUNK : (pair + 1) * CHUNK].rearrange("p (b u) -> p b u", u=2),
                 in_=x_t[:].rearrange("p u b -> p b u"),
             )
@@ -179,17 +203,20 @@ def tile_infovae_pa_t_kernel(
                 leaky(nc, h_mu_grouped[c][:], y_mu[c][:].rearrange("p m b -> p b m"))
 
         def group_h_sig(c):
-            if live(c):
-                h_sig_grouped[c] = one.tile([P, CHUNK, PACK], BF16, name="h_sig_grouped", align_bytes=64)
+            if not live(c):
+                return
+            h_sig_grouped[c] = one.tile([P, CHUNK, PACK], BF16, name="h_sig_grouped", align_bytes=64)
+            if c == 0:
+                to_v, from_v = side_by_side(h_sig[c], h_sig_grouped[c], slice(0, GPSIMD_COLS))
+                nc.vector.tensor_copy(out=to_v, in_=from_v)
+            else:
                 nc.gpsimd.tensor_scalar(
                     out=h_sig_grouped[c][:, 0:GPSIMD_COLS, :],
                     in0=h_sig[c][:, :, 0:GPSIMD_COLS].rearrange("p m b -> p b m"),
                     scalar1=1.0, scalar2=0.0, op0=ALU.mult, op1=ALU.add,
                 )
-                nc.scalar.copy(
-                    out=h_sig_grouped[c][:, GPSIMD_COLS:CHUNK, :].rearrange("p (c i) j -> p c j i", i=4),
-                    in_=h_sig[c][:, :, GPSIMD_COLS:CHUNK].rearrange("p j (c i) -> p c j i", i=4),
-                )
+            to_s, from_s = side_by_side(h_sig[c], h_sig_grouped[c], slice(GPSIMD_COLS, CHUNK))
+            nc.scalar.copy(out=to_s, in_=from_s)
 
         def quantise_h_mu(c):
             if live(c):
@@ -267,7 +294,19 @@ def tile_infovae_pa_t_kernel(
                     nc.sync.dma_start(out=out_chunks[s][c], in_=z[c][:, s, :])
 
 
-        load_x(0)
+        w1_mu_raw = load_weight(nc, stage, w1_mu, HIDDEN, "w1_mu")
+        load_x(0, parts=2)
+        b1_mu_raw = load_bias(nc, stage, b1_mu, HIDDEN_TILES, "b1_mu")
+        w1_sig_raw = load_weight(nc, stage, w1_sig, HIDDEN, "w1_sig")
+        b1_sig_raw = load_bias(nc, stage, b1_sig, HIDDEN_TILES, "b1_sig")
+        load_x(1)
+        w2_mu_raw = load_weight(nc, stage, w2_mu, LATENT, "w2_mu")
+        b2_mu_raw = load_bias(nc, stage, b2_mu, 1, "b2_mu")
+        w2_sig_raw = load_weight(nc, stage, w2_sig, LATENT, "w2_sig")
+        b2_sig_raw = load_bias(nc, stage, b2_sig, 1, "b2_sig")
+        load_x(2)
+        load_noise(0)
+
         identity = keep.tile([P, P], F32, name="identity")
         make_identity(nc, identity[:])
         zero = keep.tile([P, 1], F32, name="zero")
@@ -275,33 +314,40 @@ def tile_infovae_pa_t_kernel(
         warm = keep.tile([P, 1], F32, name="warm")
         nc.scalar.activation(out=warm[:], in_=zero[:], func=ACT.Tanh)
 
-        w1_mu_q = quantise_weight(nc, stage, keep, w1_mu, HIDDEN, "w1_mu", True)
-        b1_mu_f = load_bias(nc, stage, keep, b1_mu, HIDDEN_TILES, "b1_mu")
         turn_x(0, 0)
-        turn_x(0, 1)
+        turn_x(0, 1, pool=psum_h, bank="acc")
+        w1_mu_grouped = group_weight(nc, stage, w1_mu_raw, "w1_mu", True)
+        b1_mu_f = scaled_bias(nc, keep, b1_mu_raw, 1.0, "b1_mu")
+        w1_mu_q = quantise_weight(nc, keep, w1_mu_grouped, "w1_mu")
         quantise_x(0)
-        w1_sig_q = quantise_weight(nc, stage, keep, w1_sig, HIDDEN, "w1_sig", True)
-        b1_sig_f = load_bias(nc, stage, keep, b1_sig, HIDDEN_TILES, "b1_sig")
-        load_x(1)
-        load_x(2)
-        w2_mu_q = quantise_weight(nc, stage, keep, w2_mu, LATENT, "w2_mu", False)
-        b2_mu_f = load_bias(nc, stage, keep, b2_mu, 1, "b2_mu")
-        b2_mu_flat = keep.tile([P, 1], F32, name="b2_mu_flat")
-        nc.vector.tensor_scalar(out=b2_mu_flat[:], in0=b2_mu_f[:], scalar1=NEG_SLOPE, scalar2=None, op0=ALU.mult)
-        w2_sig_q = quantise_weight(nc, stage, keep, w2_sig, LATENT, "w2_sig", False)
-        b2_sig_f = load_bias(nc, stage, keep, b2_sig, 1, "b2_sig")
-        b2_sig_steep = keep.tile([P, 1], F32, name="b2_sig_steep")
-        nc.vector.tensor_scalar(out=b2_sig_steep[:], in0=b2_sig_f[:], scalar1=0.5, scalar2=None, op0=ALU.mult)
-        b2_sig_flat = keep.tile([P, 1], F32, name="b2_sig_flat")
-        nc.vector.tensor_scalar(
-            out=b2_sig_flat[:], in0=b2_sig_f[:], scalar1=0.5 * NEG_SLOPE, scalar2=None, op0=ALU.mult
-        )
-        load_noise(0)
-        turn_x(1, 0)
-        turn_x(1, 1)
-        quantise_x(1)
+        w1_sig_grouped = group_weight(nc, stage, w1_sig_raw, "w1_sig", True)
+        b1_sig_f = scaled_bias(nc, keep, b1_sig_raw, 1.0, "b1_sig")
+        w1_sig_q = quantise_weight(nc, keep, w1_sig_grouped, "w1_sig")
 
-        for i in range(N_CHUNKS + 2):
+        load_x(3)
+        load_noise(1)
+        hidden_mu(0)
+        turn_x(1, 0, copy=nc.vector.tensor_copy)
+        hidden_sig(0)
+        turn_x(1, 1, pool=psum_o, bank="std")
+        group_h_mu(0)
+        quantise_x(1)
+        group_h_sig(0)
+        turn_x(2, 0)
+        turn_x(2, 1, pool=psum_o, bank="mean")
+        quantise_h_mu(0)
+        w2_mu_grouped = group_weight(nc, stage, w2_mu_raw, "w2_mu", False)
+        w2_sig_grouped = group_weight(nc, stage, w2_sig_raw, "w2_sig", False)
+        w2_mu_q = quantise_weight(nc, keep, w2_mu_grouped, "w2_mu")
+        w2_sig_q = quantise_weight(nc, keep, w2_sig_grouped, "w2_sig")
+        b2_mu_f = scaled_bias(nc, keep, b2_mu_raw, 1.0, "b2_mu")
+        b2_mu_flat = scaled_bias(nc, keep, b2_mu_raw, NEG_SLOPE, "b2_mu_flat")
+        b2_sig_steep = scaled_bias(nc, keep, b2_sig_raw, 0.5, "b2_sig_steep")
+        b2_sig_flat = scaled_bias(nc, keep, b2_sig_raw, 0.5 * NEG_SLOPE, "b2_sig_flat")
+        quantise_x(2)
+        quantise_h_sig(0)
+
+        for i in range(1, N_CHUNKS + 2):
             load_x(i + 3)
             load_noise(i + 1)
             hidden_mu(i)
@@ -309,12 +355,13 @@ def tile_infovae_pa_t_kernel(
             output_mean(i - 1)
             group_h_sig(i)
             turn_back(i - 2)
-            turn_x(i + 2, 0)
-            output_std(i - 1)
-            turn_x(i + 2, 1)
             group_h_mu(i)
             scale_noise(i - 2)
+            x_copy = nc.vector.tensor_copy if i == 1 else nc.scalar.copy
+            turn_x(i + 2, 0, copy=x_copy)
             leaky_mean(i - 1)
+            output_std(i - 1)
+            turn_x(i + 2, 1, copy=x_copy)
             add_mean(i - 2)
             quantise_h_mu(i)
             std_dev(i - 1)

@@ -23,8 +23,6 @@ NEG_SLOPE = 0.01
 LV_MIN, LV_MAX = -10.0, 10.0
 STD_MIN, STD_MAX = math.exp(0.5 * LV_MIN), math.exp(0.5 * LV_MAX)
 
-GPSIMD_COLS = 384
-
 FLOPS = 2 * BATCH * 2 * (FEATURES * HIDDEN + HIDDEN * LATENT)
 
 
@@ -98,13 +96,6 @@ def leaky(nc, out, y):
     nc.vector.scalar_tensor_tensor(out=out, in0=y, scalar=NEG_SLOPE, in1=y, op0=ALU.mult, op1=ALU.max)
 
 
-def side_by_side(planes, grouped, cols):
-    return (
-        grouped[:, cols, :].rearrange("p (c i) j -> p c j i", i=4),
-        planes[:, :, cols].rearrange("p j (c i) -> p c j i", i=4),
-    )
-
-
 def tile_infovae_pa_t_kernel(
     tc, x, noise_enc, noise_z, w1_mu, b1_mu, w2_mu, b2_mu, w1_sig, b1_sig, w2_sig, b2_sig, out_0, out_1
 ):
@@ -156,6 +147,7 @@ def tile_infovae_pa_t_kernel(
             if pair == 0:
                 x_grouped[c] = two.tile([P, CHUNK, PACK], BF16, name="x_grouped", align_bytes=64)
             x_grouped_words = x_grouped[c][:].rearrange("p b j -> p (b j)").bitcast(F32)
+            x_grouped_words = x_grouped_words.rearrange("p (r t u) -> p r t u", t=ROW_TILES, u=2)
             words = FEATURES // 2
             x_t = pool.tile([P, 2, CHUNK // 2], F32, name=bank)
             for tt in range(2):
@@ -167,8 +159,8 @@ def tile_infovae_pa_t_kernel(
                         identity[:],
                     )
             copy(
-                out=x_grouped_words[:, pair * CHUNK : (pair + 1) * CHUNK].rearrange("p (b u) -> p b u", u=2),
-                in_=x_t[:].rearrange("p u b -> p b u"),
+                out=x_grouped_words[:, :, 2 * pair : 2 * pair + 2, :],
+                in_=x_t[:].rearrange("p u (t r) -> p r t u", t=2),
             )
 
         def quantise_x(c):
@@ -178,12 +170,16 @@ def tile_infovae_pa_t_kernel(
         def hidden_mu(c):
             if not live(c):
                 return
-            y_mu[c] = two.tile([P, HIDDEN_TILES, CHUNK], F32, name="y_mu")
+            y_mu[c] = two.tile([P, CHUNK // ROW_TILES, HIDDEN_TILES, ROW_TILES], F32, name="y_mu")
             for m in range(HIDDEN_TILES):
                 acc = psum_h.tile([P, CHUNK], F32, name="acc")
                 mx_pass(nc, acc, w1_mu_q, slice(m * P, (m + 1) * P), x_q[c])
                 nc.scalar.activation(
-                    out=y_mu[c][:, m, :], in_=acc[:], func=ACT.Identity, bias=b1_mu_f[:, m : m + 1], scale=1.0
+                    out=y_mu[c][:, :, m, :],
+                    in_=acc[:].rearrange("p (r t) -> p r t", t=ROW_TILES),
+                    func=ACT.Identity,
+                    bias=b1_mu_f[:, m : m + 1],
+                    scale=1.0,
                 )
 
         def hidden_sig(c):
@@ -200,23 +196,27 @@ def tile_infovae_pa_t_kernel(
         def group_h_mu(c):
             if live(c):
                 h_mu_grouped[c] = two.tile([P, CHUNK, PACK], BF16, name="h_mu_grouped", align_bytes=64)
-                leaky(nc, h_mu_grouped[c][:], y_mu[c][:].rearrange("p m b -> p b m"))
+                streams = h_mu_grouped[c][:].rearrange("p b j -> p (b j)")
+                leaky(
+                    nc,
+                    streams.rearrange("p (t q) -> p q t", t=ROW_TILES),
+                    y_mu[c][:].rearrange("p r m t -> p (r m) t"),
+                )
 
         def group_h_sig(c):
             if not live(c):
                 return
             h_sig_grouped[c] = one.tile([P, CHUNK, PACK], BF16, name="h_sig_grouped", align_bytes=64)
             if c == 0:
-                to_v, from_v = side_by_side(h_sig[c], h_sig_grouped[c], slice(0, GPSIMD_COLS))
-                nc.vector.tensor_copy(out=to_v, in_=from_v)
+                nc.vector.tensor_copy(
+                    out=h_sig_grouped[c][:].rearrange("p (b i) j -> p b j i", i=4),
+                    in_=h_sig[c][:].rearrange("p j (b i) -> p b j i", i=4),
+                )
             else:
                 nc.gpsimd.tensor_scalar(
-                    out=h_sig_grouped[c][:, 0:GPSIMD_COLS, :],
-                    in0=h_sig[c][:, :, 0:GPSIMD_COLS].rearrange("p m b -> p b m"),
+                    out=h_sig_grouped[c][:], in0=h_sig[c][:].rearrange("p m b -> p b m"),
                     scalar1=1.0, scalar2=0.0, op0=ALU.mult, op1=ALU.add,
                 )
-            to_s, from_s = side_by_side(h_sig[c], h_sig_grouped[c], slice(GPSIMD_COLS, CHUNK))
-            nc.scalar.copy(out=to_s, in_=from_s)
 
         def quantise_h_mu(c):
             if live(c):
@@ -243,12 +243,18 @@ def tile_infovae_pa_t_kernel(
             e_flat[c] = two.tile([P, CHUNK], F32, name="e_flat")
             acc = psum_o.tile([P, CHUNK], F32, name="acc_std")
             mx_pass(nc, acc, w2_sig_q, slice(0, LATENT), h_sig_q[c])
-            nc.scalar.activation(
-                out=e_steep[c][:], in_=acc[:], func=ACT.Exp, bias=b2_sig_steep[:, 0:1], scale=0.5
-            )
-            nc.scalar.activation(
-                out=e_flat[c][:], in_=acc[:], func=ACT.Exp, bias=b2_sig_flat[:, 0:1], scale=0.5 * NEG_SLOPE
-            )
+            u_turned = acc[:].rearrange("p (r t) -> p t r", t=ROW_TILES)
+            for e, bias, scale in (
+                (e_steep[c], b2_sig_steep, 0.5),
+                (e_flat[c], b2_sig_flat, 0.5 * NEG_SLOPE),
+            ):
+                nc.scalar.activation(
+                    out=e[:].rearrange("p (t r) -> p t r", t=ROW_TILES),
+                    in_=u_turned,
+                    func=ACT.Exp,
+                    bias=bias[:, 0:1],
+                    scale=scale,
+                )
 
         def leaky_mean(c):
             if live(c):
@@ -344,7 +350,6 @@ def tile_infovae_pa_t_kernel(
         b2_mu_flat = scaled_bias(nc, keep, b2_mu_raw, NEG_SLOPE, "b2_mu_flat")
         b2_sig_steep = scaled_bias(nc, keep, b2_sig_raw, 0.5, "b2_sig_steep")
         b2_sig_flat = scaled_bias(nc, keep, b2_sig_raw, 0.5 * NEG_SLOPE, "b2_sig_flat")
-        quantise_x(2)
         quantise_h_sig(0)
 
         for i in range(1, N_CHUNKS + 2):
@@ -356,6 +361,7 @@ def tile_infovae_pa_t_kernel(
             group_h_sig(i)
             turn_back(i - 2)
             group_h_mu(i)
+            quantise_x(i + 1)
             scale_noise(i - 2)
             x_copy = nc.vector.tensor_copy if i == 1 else nc.scalar.copy
             turn_x(i + 2, 0, copy=x_copy)
@@ -365,5 +371,4 @@ def tile_infovae_pa_t_kernel(
             add_mean(i - 2)
             quantise_h_mu(i)
             std_dev(i - 1)
-            quantise_x(i + 2)
             quantise_h_sig(i)

@@ -18,6 +18,7 @@ BATCH, FEATURES, HIDDEN, LATENT = 8192, 512, 512, 128
 CHUNK = 512
 ROW_TILES = CHUNK // P
 N_CHUNKS = BATCH // CHUNK
+LAST = N_CHUNKS - 1
 HIDDEN_TILES = HIDDEN // P
 NEG_SLOPE = 0.01
 LV_MIN, LV_MAX = -10.0, 10.0
@@ -282,21 +283,24 @@ def tile_infovae_pa_t_kernel(
                     cols = slice(t * P, (t + 1) * P)
                     nc.tensor.transpose(back[:, cols], turned[:, cols], identity[:])
 
-        def scale_noise(c):
+        def scale_noise(c, samples=slice(0, 2)):
             if live(c):
-                z[c] = three.tile([P, 2, CHUNK], F32, name="z")
+                if samples.start == 0:
+                    z[c] = three.tile([P, 2, CHUNK], F32, name="z")
+                n = samples.stop - samples.start
                 nc.vector.scalar_tensor_tensor(
-                    out=z[c][:], in0=std[c][:].unsqueeze(1).to_broadcast([P, 2, CHUNK]), scalar=STD_MAX,
-                    in1=noise[c][:], op0=ALU.min, op1=ALU.mult,
+                    out=z[c][:, samples, :], in0=std[c][:].unsqueeze(1).to_broadcast([P, n, CHUNK]),
+                    scalar=STD_MAX, in1=noise[c][:, samples, :], op0=ALU.min, op1=ALU.mult,
                 )
 
-        def add_mean(c):
+        def add_mean(c, samples=slice(0, 2)):
             if live(c):
+                n = samples.stop - samples.start
                 nc.vector.tensor_tensor(
-                    out=z[c][:], in0=z[c][:], in1=mean[c][:].unsqueeze(1).to_broadcast([P, 2, CHUNK]),
-                    op=ALU.add,
+                    out=z[c][:, samples, :], in0=z[c][:, samples, :],
+                    in1=mean[c][:].unsqueeze(1).to_broadcast([P, n, CHUNK]), op=ALU.add,
                 )
-                for s in range(2):
+                for s in range(samples.start, samples.stop):
                     nc.sync.dma_start(out=out_chunks[s][c], in_=z[c][:, s, :])
 
 
@@ -337,22 +341,23 @@ def tile_infovae_pa_t_kernel(
         hidden_sig(0)
         turn_x(1, 1, pool=psum_o, bank="std")
         group_h_mu(0)
+        w2_mu_grouped = group_weight(nc, stage, w2_mu_raw, "w2_mu", False)
+        w2_sig_grouped = group_weight(nc, stage, w2_sig_raw, "w2_sig", False)
         quantise_x(1)
         group_h_sig(0)
         turn_x(2, 0)
         turn_x(2, 1, pool=psum_o, bank="mean")
         quantise_h_mu(0)
-        w2_mu_grouped = group_weight(nc, stage, w2_mu_raw, "w2_mu", False)
-        w2_sig_grouped = group_weight(nc, stage, w2_sig_raw, "w2_sig", False)
         w2_mu_q = quantise_weight(nc, keep, w2_mu_grouped, "w2_mu")
         w2_sig_q = quantise_weight(nc, keep, w2_sig_grouped, "w2_sig")
         b2_mu_f = scaled_bias(nc, keep, b2_mu_raw, 1.0, "b2_mu")
         b2_mu_flat = scaled_bias(nc, keep, b2_mu_raw, NEG_SLOPE, "b2_mu_flat")
         b2_sig_steep = scaled_bias(nc, keep, b2_sig_raw, 0.5, "b2_sig_steep")
         b2_sig_flat = scaled_bias(nc, keep, b2_sig_raw, 0.5 * NEG_SLOPE, "b2_sig_flat")
+        quantise_x(2)
         quantise_h_sig(0)
 
-        for i in range(1, N_CHUNKS + 2):
+        for i in range(1, LAST):
             load_x(i + 3)
             load_noise(i + 1)
             hidden_mu(i)
@@ -361,7 +366,6 @@ def tile_infovae_pa_t_kernel(
             group_h_sig(i)
             turn_back(i - 2)
             group_h_mu(i)
-            quantise_x(i + 1)
             scale_noise(i - 2)
             x_copy = nc.vector.tensor_copy if i == 1 else nc.scalar.copy
             turn_x(i + 2, 0, copy=x_copy)
@@ -371,4 +375,30 @@ def tile_infovae_pa_t_kernel(
             add_mean(i - 2)
             quantise_h_mu(i)
             std_dev(i - 1)
+            quantise_x(i + 2)
             quantise_h_sig(i)
+
+        hidden_mu(LAST)
+        hidden_sig(LAST)
+        output_mean(LAST - 1)
+        group_h_sig(LAST)
+        turn_back(LAST - 2)
+        group_h_mu(LAST)
+        scale_noise(LAST - 2)
+        leaky_mean(LAST - 1)
+        output_std(LAST - 1)
+        add_mean(LAST - 2)
+        std_dev(LAST - 1)
+        turn_back(LAST - 1)
+        quantise_h_sig(LAST)
+        output_std(LAST)
+        quantise_h_mu(LAST)
+        output_mean(LAST)
+        scale_noise(LAST - 1)
+        add_mean(LAST - 1)
+        std_dev(LAST)
+        leaky_mean(LAST)
+        turn_back(LAST)
+        for step in (scale_noise, add_mean):
+            for sample in range(2):
+                step(LAST, slice(sample, sample + 1))

@@ -114,8 +114,7 @@ def tile_infovae_pa_t_kernel(
         two = ctx.enter_context(tc.tile_pool(name="two", bufs=2))
         three = ctx.enter_context(tc.tile_pool(name="three", bufs=3))
         six = ctx.enter_context(tc.tile_pool(name="six", bufs=6))
-        psum_x = ctx.enter_context(tc.psum_pool(name="psum_x", bufs=1))
-        psum_h = ctx.enter_context(tc.psum_pool(name="psum_h", bufs=3))
+        psum_h = ctx.enter_context(tc.psum_pool(name="psum_h", bufs=4))
         psum_o = ctx.enter_context(tc.psum_pool(name="psum_o", bufs=1))
         ctx.enter_context(tc.manual_schedule())
 
@@ -141,7 +140,7 @@ def tile_infovae_pa_t_kernel(
                 for s in range(2):
                     nc.sync.dma_start(out=noise[c][:, s, :], in_=noise_chunks[s][c])
 
-        def turn_x(c, pair, pool=psum_x, bank="x_t", copy=nc.scalar.copy):
+        def turn_x(c, pair, copy=nc.scalar.copy):
             if not live(c):
                 return
             x_words = x_rows[c][:].bitcast(F32)
@@ -150,7 +149,7 @@ def tile_infovae_pa_t_kernel(
             x_grouped_words = x_grouped[c][:].rearrange("p b j -> p (b j)").bitcast(F32)
             x_grouped_words = x_grouped_words.rearrange("p (r t u) -> p r t u", t=ROW_TILES, u=2)
             words = FEATURES // 2
-            x_t = pool.tile([P, 2, CHUNK // 2], F32, name=bank)
+            x_t = psum_h.tile([P, 2, CHUNK // 2], F32, name="acc")
             for tt in range(2):
                 t = 2 * pair + tt
                 for u in range(2):
@@ -325,7 +324,7 @@ def tile_infovae_pa_t_kernel(
         nc.scalar.activation(out=warm[:], in_=zero[:], func=ACT.Tanh)
 
         turn_x(0, 0)
-        turn_x(0, 1, pool=psum_h, bank="acc")
+        turn_x(0, 1)
         w1_mu_grouped = group_weight(nc, stage, w1_mu_raw, "w1_mu", True)
         b1_mu_f = scaled_bias(nc, keep, b1_mu_raw, 1.0, "b1_mu")
         w1_mu_q = quantise_weight(nc, keep, w1_mu_grouped, "w1_mu")
@@ -339,14 +338,14 @@ def tile_infovae_pa_t_kernel(
         hidden_mu(0)
         turn_x(1, 0, copy=nc.vector.tensor_copy)
         hidden_sig(0)
-        turn_x(1, 1, pool=psum_o, bank="std")
+        turn_x(1, 1)
         group_h_mu(0)
         w2_mu_grouped = group_weight(nc, stage, w2_mu_raw, "w2_mu", False)
         w2_sig_grouped = group_weight(nc, stage, w2_sig_raw, "w2_sig", False)
         quantise_x(1)
         group_h_sig(0)
         turn_x(2, 0)
-        turn_x(2, 1, pool=psum_o, bank="mean")
+        turn_x(2, 1)
         quantise_h_mu(0)
         w2_mu_q = quantise_weight(nc, keep, w2_mu_grouped, "w2_mu")
         w2_sig_q = quantise_weight(nc, keep, w2_sig_grouped, "w2_sig")
@@ -362,9 +361,9 @@ def tile_infovae_pa_t_kernel(
             load_noise(i + 1)
             hidden_mu(i)
             hidden_sig(i)
-            output_mean(i - 1)
             group_h_sig(i)
             turn_back(i - 2)
+            output_mean(i - 1)
             group_h_mu(i)
             scale_noise(i - 2)
             x_copy = nc.vector.tensor_copy if i == 1 else nc.scalar.copy
@@ -380,9 +379,9 @@ def tile_infovae_pa_t_kernel(
 
         hidden_mu(LAST)
         hidden_sig(LAST)
-        output_mean(LAST - 1)
         group_h_sig(LAST)
         turn_back(LAST - 2)
+        output_mean(LAST - 1)
         group_h_mu(LAST)
         scale_noise(LAST - 2)
         leaky_mean(LAST - 1)

@@ -22,7 +22,7 @@ LAST = N_CHUNKS - 1
 HIDDEN_TILES = HIDDEN // P
 NEG_SLOPE = 0.01
 LV_MIN, LV_MAX = -10.0, 10.0
-STD_MIN, STD_MAX = math.exp(0.5 * LV_MIN), math.exp(0.5 * LV_MAX)
+STD_MAX = math.exp(0.5 * LV_MAX)
 
 FLOPS = 2 * BATCH * 2 * (FEATURES * HIDDEN + HIDDEN * LATENT)
 
@@ -64,9 +64,11 @@ def load_bias(nc, stage, b, per_partition, name):
     return raw
 
 
-def scaled_bias(nc, keep, raw, scale, name):
+def scaled_bias(nc, keep, raw, scale, name, add=0.0):
     bias = keep.tile([P, raw.shape[1]], F32, name=name)
-    nc.vector.tensor_scalar(out=bias[:], in0=raw[:], scalar1=scale, scalar2=None, op0=ALU.mult)
+    nc.vector.tensor_scalar(
+        out=bias[:], in0=raw[:], scalar1=scale, scalar2=add, op0=ALU.mult, op1=ALU.add
+    )
     return bias
 
 
@@ -120,7 +122,7 @@ def tile_infovae_pa_t_kernel(
 
         x_rows, noise, x_grouped, x_q, y_mu, h_sig = {}, {}, {}, {}, {}, {}
         h_mu_grouped, h_sig_grouped, h_mu_q, h_sig_q = {}, {}, {}, {}
-        acc_mean, flat, l_out, e_steep, e_flat, std_t, mean, std, z = {}, {}, {}, {}, {}, {}, {}, {}, {}
+        acc_mean, flat, l_out, acc_lv, lv_floor, lv, std_t, mean, std, z = {}, {}, {}, {}, {}, {}, {}, {}, {}, {}
 
         def live(c):
             return 0 <= c < N_CHUNKS
@@ -167,7 +169,7 @@ def tile_infovae_pa_t_kernel(
             if live(c):
                 x_q[c] = quantise(nc, three, x_grouped[c], "x")
 
-        def hidden_mu(c):
+        def hidden_mu(c, halfway=None):
             if not live(c):
                 return
             y_mu[c] = two.tile([P, CHUNK // ROW_TILES, HIDDEN_TILES, ROW_TILES], F32, name="y_mu")
@@ -181,6 +183,8 @@ def tile_infovae_pa_t_kernel(
                     bias=b1_mu_f[:, m : m + 1],
                     scale=1.0,
                 )
+                if halfway and m == HIDDEN_TILES // 2 - 1:
+                    halfway()
 
         def hidden_sig(c):
             if not live(c):
@@ -236,24 +240,31 @@ def tile_infovae_pa_t_kernel(
                 out=flat[c][:], in_=acc_mean[c][:], func=ACT.Identity, bias=b2_mu_flat[:, 0:1], scale=NEG_SLOPE
             )
 
-        def output_std(c):
+        def output_log_var(c):
             if not live(c):
                 return
-            e_steep[c] = two.tile([P, CHUNK], F32, name="e_steep")
-            e_flat[c] = two.tile([P, CHUNK], F32, name="e_flat")
-            acc = psum_o.tile([P, CHUNK], F32, name="acc_std")
-            mx_pass(nc, acc, w2_sig_q, slice(0, LATENT), h_sig_q[c])
-            u_turned = acc[:].rearrange("p (r t) -> p t r", t=ROW_TILES)
-            for e, bias, scale in (
-                (e_steep[c], b2_sig_steep, 0.5),
-                (e_flat[c], b2_sig_flat, 0.5 * NEG_SLOPE),
-            ):
+            acc_lv[c] = psum_o.tile([P, CHUNK], F32, name="acc_lv")
+            mx_pass(nc, acc_lv[c], w2_sig_q, slice(0, LATENT), h_sig_q[c])
+            lv_floor[c] = two.tile([P, ROW_TILES, P], F32, name="lv_floor")
+            nc.scalar.activation(
+                out=lv_floor[c][:], in_=acc_lv[c][:].rearrange("p (r t) -> p t r", t=ROW_TILES),
+                func=ACT.Relu, bias=b2_sig_floor[:, 0:1], scale=NEG_SLOPE,
+            )
+
+        def leaky_log_var(c):
+            if live(c):
+                lv[c] = two.tile([P, ROW_TILES, P], F32, name="lv")
+                nc.vector.scalar_tensor_tensor(
+                    out=lv[c][:], in0=acc_lv[c][:].rearrange("p (r t) -> p t r", t=ROW_TILES),
+                    scalar=b2_sig_up[:, 0:1], in1=lv_floor[c][:], op0=ALU.add, op1=ALU.max,
+                )
+
+        def std_dev(c):
+            if live(c):
+                std_t[c] = two.tile([P, CHUNK], F32, name="std_t")
                 nc.scalar.activation(
-                    out=e[:].rearrange("p (t r) -> p t r", t=ROW_TILES),
-                    in_=u_turned,
-                    func=ACT.Exp,
-                    bias=bias[:, 0:1],
-                    scale=scale,
+                    out=std_t[c][:], in_=lv[c][:].rearrange("p t r -> p (t r)"), func=ACT.Exp,
+                    bias=exp_shift[:, 0:1], scale=0.5,
                 )
 
         def leaky_mean(c):
@@ -262,14 +273,6 @@ def tile_infovae_pa_t_kernel(
                 nc.vector.scalar_tensor_tensor(
                     out=l_out[c][:], in0=acc_mean[c][:], scalar=b2_mu_f[:, 0:1], in1=flat[c][:],
                     op0=ALU.add, op1=ALU.max,
-                )
-
-        def std_dev(c):
-            if live(c):
-                std_t[c] = two.tile([P, CHUNK], F32, name="std_t")
-                nc.vector.scalar_tensor_tensor(
-                    out=std_t[c][:], in0=e_steep[c][:], scalar=STD_MIN, in1=e_flat[c][:],
-                    op0=ALU.max, op1=ALU.max,
                 )
 
         def turn_back(c):
@@ -351,15 +354,17 @@ def tile_infovae_pa_t_kernel(
         w2_sig_q = quantise_weight(nc, keep, w2_sig_grouped, "w2_sig")
         b2_mu_f = scaled_bias(nc, keep, b2_mu_raw, 1.0, "b2_mu")
         b2_mu_flat = scaled_bias(nc, keep, b2_mu_raw, NEG_SLOPE, "b2_mu_flat")
-        b2_sig_steep = scaled_bias(nc, keep, b2_sig_raw, 0.5, "b2_sig_steep")
-        b2_sig_flat = scaled_bias(nc, keep, b2_sig_raw, 0.5 * NEG_SLOPE, "b2_sig_flat")
+        b2_sig_up = scaled_bias(nc, keep, b2_sig_raw, 1.0, "b2_sig_up", add=-LV_MIN)
+        b2_sig_floor = scaled_bias(nc, keep, b2_sig_raw, NEG_SLOPE, "b2_sig_floor", add=-LV_MIN)
+        exp_shift = keep.tile([P, 1], F32, name="exp_shift")
+        nc.vector.memset(exp_shift[:], 0.5 * LV_MIN)
         quantise_x(2)
         quantise_h_sig(0)
 
         for i in range(1, LAST):
             load_x(i + 3)
             load_noise(i + 1)
-            hidden_mu(i)
+            hidden_mu(i, halfway=lambda: std_dev(i - 2))
             hidden_sig(i)
             group_h_sig(i)
             turn_back(i - 2)
@@ -369,33 +374,35 @@ def tile_infovae_pa_t_kernel(
             x_copy = nc.vector.tensor_copy if i == 1 else nc.scalar.copy
             turn_x(i + 2, 0, copy=x_copy)
             leaky_mean(i - 1)
-            output_std(i - 1)
+            output_log_var(i - 1)
             turn_x(i + 2, 1, copy=x_copy)
+            leaky_log_var(i - 1)
             add_mean(i - 2)
             quantise_h_mu(i)
-            std_dev(i - 1)
             quantise_x(i + 2)
             quantise_h_sig(i)
 
-        hidden_mu(LAST)
+        hidden_mu(LAST, halfway=lambda: std_dev(LAST - 2))
         hidden_sig(LAST)
         group_h_sig(LAST)
         turn_back(LAST - 2)
         output_mean(LAST - 1)
+        output_log_var(LAST - 1)
         group_h_mu(LAST)
         scale_noise(LAST - 2)
         leaky_mean(LAST - 1)
-        output_std(LAST - 1)
-        add_mean(LAST - 2)
+        leaky_log_var(LAST - 1)
         std_dev(LAST - 1)
+        add_mean(LAST - 2)
         turn_back(LAST - 1)
         quantise_h_sig(LAST)
-        output_std(LAST)
+        output_log_var(LAST)
         quantise_h_mu(LAST)
         output_mean(LAST)
         scale_noise(LAST - 1)
-        add_mean(LAST - 1)
+        leaky_log_var(LAST)
         std_dev(LAST)
+        add_mean(LAST - 1)
         leaky_mean(LAST)
         turn_back(LAST)
         for step in (scale_noise, add_mean):

import math
from contextlib import ExitStack

import concourse.mybir as mybir
from concourse.masks import make_identity

F32 = mybir.dt.float32
BF16 = mybir.dt.bfloat16
U32 = mybir.dt.uint32
U8 = mybir.dt.uint8
FP8X4 = mybir.dt.float8_e4m3fn_x4
ACT = mybir.ActivationFunctionType
ALU = mybir.AluOpType

P = 128
PACK = 4
BATCH, FEATURES, HIDDEN, LATENT = 8192, 512, 512, 128
CHUNK = 512
ROW_TILES = CHUNK // P
N_CHUNKS = BATCH // CHUNK
LAST = N_CHUNKS - 1
HIDDEN_TILES = HIDDEN // P
NEG_SLOPE = 0.01
LV_MIN, LV_MAX = -10.0, 10.0
STD_MAX = math.exp(0.5 * LV_MAX)

FLOPS = 2 * BATCH * 2 * (FEATURES * HIDDEN + HIDDEN * LATENT)


def load_weight(nc, stage, w, cols, name):
    raw = stage.tile([P, PACK, cols], BF16, name=name + "_raw")
    nc.sync.dma_start(out=raw[:], in_=w.rearrange("(p j) n -> p j n", j=PACK))
    return raw


def group_weight(nc, stage, raw, name, spread):
    cols = raw.shape[2]
    grouped = stage.tile([P, cols, PACK], BF16, name=name + "_grouped", align_bytes=64)
    if spread:
        nc.vector.tensor_copy(
            out=grouped[:].rearrange("p (m q) j -> p m q j", q=P),
            in_=raw[:].rearrange("p j (q m) -> p m q j", q=P),
        )
    else:
        nc.vector.tensor_copy(out=grouped[:], in_=raw[:].rearrange("p j n -> p n j"))
    return grouped


def quantise_weight(nc, keep, grouped, name):
    cols = grouped.shape[1]
    codes = keep.tile([P, cols], U32, name=name + "_codes", align_bytes=64)
    scales = keep.tile([P, cols], U8, name=name + "_scales", align_bytes=64)
    nc.vector.quantize_mx(
        out=codes[:].bitcast(FP8X4),
        scales=scales[:],
        in_=grouped[:].rearrange("p n j -> p (n j)"),
    )
    return codes, scales


def load_bias(nc, stage, b, per_partition, name):
    raw = stage.tile([P, per_partition], BF16, name=name + "_raw")
    nc.sync.dma_start(out=raw[:], in_=b.rearrange("(p m) -> p m", m=per_partition))
    return raw


def scaled_bias(nc, keep, raw, scale, name, add=0.0):
    bias = keep.tile([P, raw.shape[1]], F32, name=name)
    nc.vector.tensor_scalar(
        out=bias[:], in0=raw[:], scalar1=scale, scalar2=add, op0=ALU.mult, op1=ALU.add
    )
    return bias


def quantise(nc, pool, grouped, name):
    codes = pool.tile([P, CHUNK], U32, name=name + "_codes", align_bytes=64)
    scales = pool.tile([P, CHUNK], U8, name=name + "_scales", align_bytes=64)
    nc.vector.quantize_mx(
        out=codes[:].bitcast(FP8X4),
        scales=scales[:],
        in_=grouped[:].rearrange("p b j -> p (b j)"),
    )
    return codes, scales


def mx_pass(nc, acc, weight, w_cols, moving):
    nc.tensor.matmul_mx(
        out=acc[:],
        lhsT=weight[0][:, w_cols].bitcast(FP8X4),
        lhsT_scale=weight[1][:, w_cols],
        rhs=moving[0][:].bitcast(FP8X4),
        rhs_scale=moving[1][:],
        start=True,
        stop=True,
    )


def leaky(nc, out, y):
    nc.vector.scalar_tensor_tensor(out=out, in0=y, scalar=NEG_SLOPE, in1=y, op0=ALU.mult, op1=ALU.max)


def tile_infovae_pa_t_kernel(
    tc, x, noise_enc, noise_z, w1_mu, b1_mu, w2_mu, b2_mu, w1_sig, b1_sig, w2_sig, b2_sig, out_0, out_1
):
    nc = tc.nc
    x_chunks = x.rearrange("(p c t) k -> c p (t k)", c=N_CHUNKS, t=ROW_TILES)
    noise_chunks = [
        n.rearrange("(p c t) h -> c p (t h)", c=N_CHUNKS, t=ROW_TILES) for n in (noise_enc, noise_z)
    ]
    out_chunks = [o.rearrange("(p c t) h -> c p (t h)", c=N_CHUNKS, t=ROW_TILES) for o in (out_0, out_1)]

    with ExitStack() as ctx:
        keep = ctx.enter_context(tc.tile_pool(name="keep", bufs=1))
        stage = ctx.enter_context(tc.tile_pool(name="stage", bufs=1))
        one = ctx.enter_context(tc.tile_pool(name="one", bufs=1))
        two = ctx.enter_context(tc.tile_pool(name="two", bufs=2))
        three = ctx.enter_context(tc.tile_pool(name="three", bufs=3))
        six = ctx.enter_context(tc.tile_pool(name="six", bufs=6))
        psum_h = ctx.enter_context(tc.psum_pool(name="psum_h", bufs=4))
        psum_o = ctx.enter_context(tc.psum_pool(name="psum_o", bufs=1))
        ctx.enter_context(tc.manual_schedule())

        x_rows, noise, x_grouped, x_q, y_mu, h_sig = {}, {}, {}, {}, {}, {}
        h_mu_grouped, h_sig_grouped, h_mu_q, h_sig_q = {}, {}, {}, {}
        acc_mean, flat, l_out, acc_lv, lv_floor, lv, std_t, mean, std, z = {}, {}, {}, {}, {}, {}, {}, {}, {}, {}

        def live(c):
            return 0 <= c < N_CHUNKS


        def load_x(c, parts=1):
            if live(c):
                x_rows[c] = three.tile([P, ROW_TILES * FEATURES], BF16, name="x_rows")
                width = ROW_TILES * FEATURES // parts
                for k in range(parts):
                    part = slice(k * width, (k + 1) * width)
                    nc.sync.dma_start(out=x_rows[c][:, part], in_=x_chunks[c][:, part])

        def load_noise(c):
            if live(c):
                noise[c] = six.tile([P, 2, CHUNK], BF16, name="noise")
                for s in range(2):
                    nc.sync.dma_start(out=noise[c][:, s, :], in_=noise_chunks[s][c])

        def turn_x(c, pair, copy=nc.scalar.copy):
            if not live(c):
                return
            x_words = x_rows[c][:].bitcast(F32)
            if pair == 0:
                x_grouped[c] = two.tile([P, CHUNK, PACK], BF16, name="x_grouped", align_bytes=64)
            x_grouped_words = x_grouped[c][:].rearrange("p b j -> p (b j)").bitcast(F32)
            x_grouped_words = x_grouped_words.rearrange("p (r t u) -> p r t u", t=ROW_TILES, u=2)
            words = FEATURES // 2
            x_t = psum_h.tile([P, 2, CHUNK // 2], F32, name="acc")
            for tt in range(2):
                t = 2 * pair + tt
                for u in range(2):
                    nc.tensor.transpose(
                        x_t[:, u, tt * P : (tt + 1) * P],
                        x_words[:, t * words + u : (t + 1) * words : 2],
                        identity[:],
                    )
            copy(
                out=x_grouped_words[:, :, 2 * pair : 2 * pair + 2, :],
                in_=x_t[:].rearrange("p u (t r) -> p r t u", t=2),
            )

        def quantise_x(c):
            if live(c):
                x_q[c] = quantise(nc, three, x_grouped[c], "x")

        def hidden_mu(c, halfway=None):
            if not live(c):
                return
            y_mu[c] = two.tile([P, CHUNK // ROW_TILES, HIDDEN_TILES, ROW_TILES], F32, name="y_mu")
            for m in range(HIDDEN_TILES):
                acc = psum_h.tile([P, CHUNK], F32, name="acc")
                mx_pass(nc, acc, w1_mu_q, slice(m * P, (m + 1) * P), x_q[c])
                nc.scalar.activation(
                    out=y_mu[c][:, :, m, :],
                    in_=acc[:].rearrange("p (r t) -> p r t", t=ROW_TILES),
                    func=ACT.Identity,
                    bias=b1_mu_f[:, m : m + 1],
                    scale=1.0,
                )
                if halfway and m == HIDDEN_TILES // 2 - 1:
                    halfway()

        def hidden_sig(c):
            if not live(c):
                return
            h_sig[c] = two.tile([P, HIDDEN_TILES, CHUNK], BF16, name="h_sig")
            for m in range(HIDDEN_TILES):
                acc = psum_h.tile([P, CHUNK], F32, name="acc")
                mx_pass(nc, acc, w1_sig_q, slice(m * P, (m + 1) * P), x_q[c])
                nc.scalar.activation(
                    out=h_sig[c][:, m, :], in_=acc[:], func=ACT.Tanh, bias=b1_sig_f[:, m : m + 1], scale=1.0
                )

        def group_h_mu(c):
            if live(c):
                h_mu_grouped[c] = two.tile([P, CHUNK, PACK], BF16, name="h_mu_grouped", align_bytes=64)
                streams = h_mu_grouped[c][:].rearrange("p b j -> p (b j)")
                leaky(
                    nc,
                    streams.rearrange("p (t q) -> p q t", t=ROW_TILES),
                    y_mu[c][:].rearrange("p r m t -> p (r m) t"),
                )

        def group_h_sig(c):
            if not live(c):
                return
            h_sig_grouped[c] = one.tile([P, CHUNK, PACK], BF16, name="h_sig_grouped", align_bytes=64)
            if c == 0:
                nc.vector.tensor_copy(
                    out=h_sig_grouped[c][:].rearrange("p (b i) j -> p b j i", i=4),
                    in_=h_sig[c][:].rearrange("p j (b i) -> p b j i", i=4),
                )
            else:
                nc.gpsimd.tensor_scalar(
                    out=h_sig_grouped[c][:], in0=h_sig[c][:].rearrange("p m b -> p b m"),
                    scalar1=1.0, scalar2=0.0, op0=ALU.mult, op1=ALU.add,
                )

        def quantise_h_mu(c):
            if live(c):
                h_mu_q[c] = quantise(nc, two, h_mu_grouped[c], "h_mu")

        def quantise_h_sig(c):
            if live(c):
                h_sig_q[c] = quantise(nc, two, h_sig_grouped[c], "h_sig")

        def output_mean(c):
            if not live(c):
                return
            acc_mean[c] = psum_o.tile([P, CHUNK], F32, name="acc_mean")
            mx_pass(nc, acc_mean[c], w2_mu_q, slice(0, LATENT), h_mu_q[c])
            flat[c] = two.tile([P, CHUNK], F32, name="flat")
            nc.scalar.activation(
                out=flat[c][:], in_=acc_mean[c][:], func=ACT.Identity, bias=b2_mu_flat[:, 0:1], scale=NEG_SLOPE
            )

        def output_log_var(c):
            if not live(c):
                return
            acc_lv[c] = psum_o.tile([P, CHUNK], F32, name="acc_lv")
            mx_pass(nc, acc_lv[c], w2_sig_q, slice(0, LATENT), h_sig_q[c])
            lv_floor[c] = two.tile([P, ROW_TILES, P], F32, name="lv_floor")
            nc.scalar.activation(
                out=lv_floor[c][:], in_=acc_lv[c][:].rearrange("p (r t) -> p t r", t=ROW_TILES),
                func=ACT.Relu, bias=b2_sig_floor[:, 0:1], scale=NEG_SLOPE,
            )

        def leaky_log_var(c):
            if live(c):
                lv[c] = two.tile([P, ROW_TILES, P], F32, name="lv")
                nc.vector.scalar_tensor_tensor(
                    out=lv[c][:], in0=acc_lv[c][:].rearrange("p (r t) -> p t r", t=ROW_TILES),
                    scalar=b2_sig_up[:, 0:1], in1=lv_floor[c][:], op0=ALU.add, op1=ALU.max,
                )

        def std_dev(c):
            if live(c):
                std_t[c] = two.tile([P, CHUNK], F32, name="std_t")
                nc.scalar.activation(
                    out=std_t[c][:], in_=lv[c][:].rearrange("p t r -> p (t r)"), func=ACT.Exp,
                    bias=exp_shift[:, 0:1], scale=0.5,
                )

        def leaky_mean(c):
            if live(c):
                l_out[c] = two.tile([P, CHUNK], F32, name="l_out")
                nc.vector.scalar_tensor_tensor(
                    out=l_out[c][:], in0=acc_mean[c][:], scalar=b2_mu_f[:, 0:1], in1=flat[c][:],
                    op0=ALU.add, op1=ALU.max,
                )

        def turn_back(c):
            if not live(c):
                return
            std[c] = psum_o.tile([P, CHUNK], F32, name="std")
            mean[c] = psum_o.tile([P, CHUNK], F32, name="mean")
            for back, turned in ((std[c], std_t[c]), (mean[c], l_out[c])):
                for t in range(ROW_TILES):
                    cols = slice(t * P, (t + 1) * P)
                    nc.tensor.transpose(back[:, cols], turned[:, cols], identity[:])

        def scale_noise(c, samples=slice(0, 2)):
            if live(c):
                if samples.start == 0:
                    z[c] = three.tile([P, 2, CHUNK], F32, name="z")
                n = samples.stop - samples.start
                nc.vector.scalar_tensor_tensor(
                    out=z[c][:, samples, :], in0=std[c][:].unsqueeze(1).to_broadcast([P, n, CHUNK]),
                    scalar=STD_MAX, in1=noise[c][:, samples, :], op0=ALU.min, op1=ALU.mult,
                )

        def add_mean(c, samples=slice(0, 2)):
            if live(c):
                n = samples.stop - samples.start
                nc.vector.tensor_tensor(
                    out=z[c][:, samples, :], in0=z[c][:, samples, :],
                    in1=mean[c][:].unsqueeze(1).to_broadcast([P, n, CHUNK]), op=ALU.add,
                )
                for s in range(samples.start, samples.stop):
                    nc.sync.dma_start(out=out_chunks[s][c], in_=z[c][:, s, :])


        w1_mu_raw = load_weight(nc, stage, w1_mu, HIDDEN, "w1_mu")
        load_x(0, parts=2)
        b1_mu_raw = load_bias(nc, stage, b1_mu, HIDDEN_TILES, "b1_mu")
        w1_sig_raw = load_weight(nc, stage, w1_sig, HIDDEN, "w1_sig")
        b1_sig_raw = load_bias(nc, stage, b1_sig, HIDDEN_TILES, "b1_sig")
        load_x(1)
        w2_mu_raw = load_weight(nc, stage, w2_mu, LATENT, "w2_mu")
        b2_mu_raw = load_bias(nc, stage, b2_mu, 1, "b2_mu")
        w2_sig_raw = load_weight(nc, stage, w2_sig, LATENT, "w2_sig")
        b2_sig_raw = load_bias(nc, stage, b2_sig, 1, "b2_sig")
        load_x(2)
        load_noise(0)

        identity = keep.tile([P, P], F32, name="identity")
        make_identity(nc, identity[:])
        zero = keep.tile([P, 1], F32, name="zero")
        nc.vector.memset(zero[:], 0.0)
        warm = keep.tile([P, 1], F32, name="warm")
        nc.scalar.activation(out=warm[:], in_=zero[:], func=ACT.Tanh)

        turn_x(0, 0)
        turn_x(0, 1)
        w1_mu_grouped = group_weight(nc, stage, w1_mu_raw, "w1_mu", True)
        b1_mu_f = scaled_bias(nc, keep, b1_mu_raw, 1.0, "b1_mu")
        w1_mu_q = quantise_weight(nc, keep, w1_mu_grouped, "w1_mu")
        quantise_x(0)
        w1_sig_grouped = group_weight(nc, stage, w1_sig_raw, "w1_sig", True)
        b1_sig_f = scaled_bias(nc, keep, b1_sig_raw, 1.0, "b1_sig")
        w1_sig_q = quantise_weight(nc, keep, w1_sig_grouped, "w1_sig")

        load_x(3)
        load_noise(1)
        hidden_mu(0)
        turn_x(1, 0, copy=nc.vector.tensor_copy)
        hidden_sig(0)
        turn_x(1, 1)
        group_h_mu(0)
        w2_mu_grouped = group_weight(nc, stage, w2_mu_raw, "w2_mu", False)
        w2_sig_grouped = group_weight(nc, stage, w2_sig_raw, "w2_sig", False)
        quantise_x(1)
        group_h_sig(0)
        turn_x(2, 0)
        turn_x(2, 1)
        quantise_h_mu(0)
        w2_mu_q = quantise_weight(nc, keep, w2_mu_grouped, "w2_mu")
        w2_sig_q = quantise_weight(nc, keep, w2_sig_grouped, "w2_sig")
        b2_mu_f = scaled_bias(nc, keep, b2_mu_raw, 1.0, "b2_mu")
        b2_mu_flat = scaled_bias(nc, keep, b2_mu_raw, NEG_SLOPE, "b2_mu_flat")
        b2_sig_up = scaled_bias(nc, keep, b2_sig_raw, 1.0, "b2_sig_up", add=-LV_MIN)
        b2_sig_floor = scaled_bias(nc, keep, b2_sig_raw, NEG_SLOPE, "b2_sig_floor", add=-LV_MIN)
        exp_shift = keep.tile([P, 1], F32, name="exp_shift")
        nc.vector.memset(exp_shift[:], 0.5 * LV_MIN)
        quantise_x(2)
        quantise_h_sig(0)

        for i in range(1, LAST):
            load_x(i + 3)
            load_noise(i + 1)
            hidden_mu(i, halfway=lambda: std_dev(i - 2))
            hidden_sig(i)
            group_h_sig(i)
            turn_back(i - 2)
            output_mean(i - 1)
            group_h_mu(i)
            scale_noise(i - 2)
            x_copy = nc.vector.tensor_copy if i == 1 else nc.scalar.copy
            turn_x(i + 2, 0, copy=x_copy)
            leaky_mean(i - 1)
            output_log_var(i - 1)
            turn_x(i + 2, 1, copy=x_copy)
            leaky_log_var(i - 1)
            add_mean(i - 2)
            quantise_h_mu(i)
            quantise_x(i + 2)
            quantise_h_sig(i)

        hidden_mu(LAST, halfway=lambda: std_dev(LAST - 2))
        hidden_sig(LAST)
        group_h_sig(LAST)
        turn_back(LAST - 2)
        output_mean(LAST - 1)
        output_log_var(LAST - 1)
        group_h_mu(LAST)
        scale_noise(LAST - 2)
        leaky_mean(LAST - 1)
        leaky_log_var(LAST - 1)
        std_dev(LAST - 1)
        add_mean(LAST - 2)
        turn_back(LAST - 1)
        quantise_h_sig(LAST)
        output_log_var(LAST)
        quantise_h_mu(LAST)
        output_mean(LAST)
        scale_noise(LAST - 1)
        leaky_log_var(LAST)
        std_dev(LAST)
        add_mean(LAST - 1)
        leaky_mean(LAST)
        turn_back(LAST)
        for step in (scale_noise, add_mean):
            for sample in range(2):
                step(LAST, slice(sample, sample + 1))
